import numpy as np
import ml_dtypes


def mxq(x, axis, fmt="e4m3"):
    dtype, down = {"e4m3": (ml_dtypes.float8_e4m3fn, 7), "e5m2": (ml_dtypes.float8_e5m2, 14)}[fmt]
    v = np.moveaxis(np.asarray(x, np.float32).astype(ml_dtypes.bfloat16).astype(np.float64), axis, -1)
    blocks = v.reshape(v.shape[:-1] + (-1, 32))
    amax = np.abs(blocks).max(-1, keepdims=True)
    byte = np.maximum(np.where(amax > 0, np.frexp(amax)[1] - 1 + 127, 0) - down, 1)
    scale = np.exp2(byte - 127.0)
    codes = (blocks / scale).astype(np.float32).astype(dtype).astype(np.float64)
    return np.moveaxis((codes * scale).reshape(v.shape), -1, axis)


WIDE = False


def mx_kscale(k):
    if not WIDE:
        return np.ones(k)
    levels = np.array([10, -10, 5, -5, 0])
    if k % 512:
        return np.exp2(np.random.permutation(np.resize(levels, k // 32))).repeat(32)
    a = np.empty((k // 512, 16))
    for p in range(k // 512):
        a[p, :8] = np.random.permutation(np.resize(levels, 8))
        for g in range(8):
            far = levels[np.abs(levels - a[p, g]) >= 10]
            a[p, g + 8] = far[np.random.randint(len(far))]
    return np.exp2(a.ravel()).repeat(32)


BF16 = ml_dtypes.bfloat16


def bf(x):
    return np.asarray(x, np.float32).astype(BF16)


def f64(x):
    return np.asarray(x).astype(np.float64)


B, N, E, L, A, H1, H2, G = 128, 8, 8, 6144, 2048, 128, 1024, 8
D = L + A
EPS = 1e-5


def mish(v):
    return v * np.tanh(np.log(1.0 + np.exp(v)))


def layer_norm(v, gamma, beta):
    mu = v.mean(-1, keepdims=True)
    var = v.var(-1, keepdims=True)
    return (v - mu) / np.sqrt(var + EPS) * gamma + beta


def setup_inputs():
    s = mx_kscale(D)
    r = np.random.standard_normal
    return {"tokens": bf(r((B, N, D)) * s),
            "logits": bf(r((B, N, E))),
            "W1": bf(r((E, D, H1)) / np.sqrt(D) / s[:, None]),
            "b1": bf(0.1 * r((E, H1))),
            "g1": bf(1.0 + 0.1 * r((E, H1))),
            "be1": bf(0.1 * r((E, H1)))}


def reference(tokens, logits, W1, b1, g1, be1):
    tok, lg = f64(tokens), f64(logits)
    ex = np.exp(lg - lg.max(1, keepdims=True))
    disp = ex / ex.sum(1, keepdims=True)
    slot = sum(disp[:, n, :].T[:, :, None] * tok[None, :, n, :] for n in range(N))
    h = (mxq(slot, 2, "e4m3") @ mxq(f64(W1), 1, "e4m3")) + f64(b1)[:, None, :]
    h = mish(layer_norm(h, f64(g1)[:, None, :], f64(be1)[:, None, :]))
    return h.transpose(1, 0, 2)

@@ -1,0 +1,239 @@
+from contextlib import ExitStack
+
+import concourse.mybir as mybir
+from concourse.masks import make_identity
+
+F32 = mybir.dt.float32
+BF16 = mybir.dt.bfloat16
+U32 = mybir.dt.uint32
+U8 = mybir.dt.uint8
+FP8X4 = mybir.dt.float8_e4m3fn_x4
+ALU = mybir.AluOpType
+ACT = mybir.ActivationFunctionType
+AXIS = mybir.AxisListType
+
+B, N, E, D, H1 = 128, 8, 8, 8192, 128
+EPS = 1e-5
+P = 128
+PACK = 4
+K_PASS = P * PACK
+CHUNK = 1024
+CHUNKS = D // CHUNK
+CHUNK_PASSES = CHUNK // K_PASS
+UNITS = E * CHUNKS
+W_UNITS = 2
+W_PASSES = W_UNITS * CHUNK_PASSES
+W_PIECES = UNITS // W_UNITS
+PAIRS = N // 2
+MISH_CLAMP = 20.0
+
+FLOPS = 2 * E * B * D * H1 + 2 * B * N * E * D
+
+
+def tile_softmoedynamics_pa_k_kernel(tc, tokens, logits, W1, b1, g1, be1, out):
+    nc = tc.nc
+    with ExitStack() as ctx:
+        const = ctx.enter_context(tc.tile_pool(name="const", bufs=1))
+        tok_pool = ctx.enter_context(tc.tile_pool(name="tok", bufs=1))
+        w_raw_pool = ctx.enter_context(tc.tile_pool(name="w_raw", bufs=3))
+        w_grp_pool = ctx.enter_context(tc.tile_pool(name="w_grp", bufs=2))
+        w_mx_pool = ctx.enter_context(tc.tile_pool(name="w_mx", bufs=3))
+        term_pool = ctx.enter_context(tc.tile_pool(name="term", bufs=8))
+        slot_pool = ctx.enter_context(tc.tile_pool(name="slot", bufs=3))
+        epi_pool = ctx.enter_context(tc.tile_pool(name="epi", bufs=2))
+        mish_pool = ctx.enter_context(tc.tile_pool(name="mish", bufs=1))
+        turned_pool = ctx.enter_context(tc.psum_pool(name="turned", bufs=7))
+        acc_pool = ctx.enter_context(tc.psum_pool(name="acc", bufs=1))
+
+        tok = [tok_pool.tile([P, N, CHUNK], BF16, name="tok%d" % c) for c in range(CHUNKS)]
+
+        def load_tokens(c, q):
+            agents = slice(2 * q, 2 * q + 2)
+            nc.sync.dma_start(
+                out=tok[c][:, agents, :], in_=tokens[:, agents, c * CHUNK : (c + 1) * CHUNK]
+            )
+
+        w_raw = {}
+        w_codes = {}
+        w_scales = {}
+
+        def load_w(piece):
+            first = piece * W_PASSES * K_PASS
+            raw = w_raw_pool.tile([P, PACK, W_PASSES * H1], BF16, name="w_raw")
+            rows = W1.rearrange("e d h -> (e d) h")[first : first + W_PASSES * K_PASS, :]
+            by_code = rows.rearrange("(g p t) h -> t p g h", t=PACK, p=P)
+            for t in range(PACK):
+                nc.sync.dma_start(
+                    out=raw[:, t, :].rearrange("p (g h) -> p g h", h=H1), in_=by_code[t]
+                )
+            w_raw[piece] = raw
+
+        def quantise_w(piece):
+            grouped = w_grp_pool.tile([P, W_PASSES * H1, PACK], BF16, name="w_grp", align_bytes=64)
+            nc.vector.tensor_copy(
+                out=grouped[:].rearrange("p (c i) t -> p c t i", i=4),
+                in_=w_raw[piece][:].rearrange("p t (c i) -> p c t i", i=4),
+            )
+            w_codes[piece] = w_mx_pool.tile([P, W_PASSES * H1], U32, name="w_codes", align_bytes=64)
+            w_scales[piece] = w_mx_pool.tile([P, W_PASSES * H1], U8, name="w_scales", align_bytes=64)
+            nc.vector.quantize_mx(
+                out=w_codes[piece][:].bitcast(FP8X4),
+                scales=w_scales[piece][:],
+                in_=grouped[:].rearrange("p w t -> p (w t)"),
+            )
+
+        lg = const.tile([P, N, E], BF16)
+        nc.sync.dma_start(out=lg[:], in_=logits)
+        for q in range(PAIRS):
+            load_tokens(0, q)
+        load_w(0)
+        for q in range(PAIRS):
+            load_tokens(1, q)
+        load_w(1)
+        for c in range(2, CHUNKS):
+            for q in range(PAIRS):
+                load_tokens(c, q)
+
+        bias_bc = const.tile([P, E * H1], BF16)
+        gain_bc = const.tile([P, E * H1], BF16)
+        shift_bc = const.tile([P, E * H1], BF16)
+        for row_bc, vec in ((bias_bc, b1), (gain_bc, g1), (shift_bc, be1)):
+            nc.gpsimd.dma_start(
+                out=row_bc[:], in_=vec.rearrange("e h -> (e h)").partition_broadcast(P)
+            )
+
+        ident = const.tile([P, P], F32)
+        make_identity(nc, ident[:])
+        minus_half = const.tile([P, 1], F32)
+        nc.vector.memset(minus_half[:], -0.5)
+        warm = const.tile([P, 1], F32)
+        nc.scalar.activation(out=warm[:], in_=minus_half[:], func=ACT.Exp)
+
+        lg_en = lg[:].rearrange("p n e -> p e n")
+        top = const.tile([P, E], F32)
+        nc.vector.tensor_reduce(out=top[:], in_=lg_en, axis=AXIS.X, op=ALU.max)
+        disp = const.tile([P, E, N], F32)
+        nc.vector.tensor_tensor(
+            out=disp[:], in0=lg_en, in1=top[:].unsqueeze(2).to_broadcast([P, E, N]), op=ALU.subtract
+        )
+        nc.scalar.activation(out=disp[:], in_=disp[:], func=ACT.Exp)
+        total = const.tile([P, E], F32)
+        nc.vector.tensor_reduce(out=total[:], in_=disp[:], axis=AXIS.X, op=ALU.add)
+        nc.vector.reciprocal(out=total[:], in_=total[:])
+        nc.vector.tensor_tensor(
+            out=disp[:], in0=disp[:], in1=total[:].unsqueeze(2).to_broadcast([P, E, N]), op=ALU.mult
+        )
+
+        quantise_w(0)
+
+        v = const.tile([P, E * H1], F32)
+
+        def layer_norm(e, acc):
+            cols = slice(e * H1, (e + 1) * H1)
+            nc.vector.tensor_tensor(out=v[:, cols], in0=acc[:], in1=bias_bc[:, cols], op=ALU.add)
+            stats = epi_pool.tile([P, 6], F32, name="stats")
+            nc.vector.bn_stats(out=stats[:], in_=v[:, cols])
+            mean_var = epi_pool.tile([P, 2], F32, name="mean_var")
+            nc.vector.bn_aggr(out=mean_var[:], in_=stats[:])
+            rstd = epi_pool.tile([P, 1], F32, name="rstd")
+            nc.gpsimd.tensor_scalar(
+                out=rstd[:], in0=mean_var[:, 1:2], scalar1=EPS, scalar2=1.0, op0=ALU.add, op1=ALU.mult
+            )
+            nc.gpsimd.tensor_tensor(out=rstd[:], in0=rstd[:], in1=minus_half[:], op=ALU.pow)
+            nc.vector.scalar_tensor_tensor(
+                out=v[:, cols], in0=v[:, cols], scalar=mean_var[:, 0:1], in1=gain_bc[:, cols],
+                op0=ALU.subtract, op1=ALU.mult,
+            )
+            nc.vector.scalar_tensor_tensor(
+                out=v[:, cols], in0=v[:, cols], scalar=rstd[:], in1=shift_bc[:, cols],
+                op0=ALU.mult, op1=ALU.add,
+            )
+
+        w = mish_pool.tile([P, E * H1], F32)
+        numer = mish_pool.tile([P, E * H1], F32)
+
+        def mish_and_store(first_e, last_e):
+            cols = slice(first_e * H1, last_e * H1)
+            nc.vector.tensor_scalar_min(out=w[:, cols], in0=v[:, cols], scalar1=MISH_CLAMP)
+            nc.scalar.activation(out=w[:, cols], in_=w[:, cols], func=ACT.Exp)
+            nc.vector.scalar_tensor_tensor(
+                out=numer[:, cols], in0=w[:, cols], scalar=2.0, in1=w[:, cols], op0=ALU.add, op1=ALU.mult
+            )
+            nc.vector.tensor_scalar_add(out=w[:, cols], in0=numer[:, cols], scalar1=2.0)
+            nc.vector.reciprocal(out=w[:, cols], in_=w[:, cols])
+            nc.vector.tensor_tensor(out=numer[:, cols], in0=numer[:, cols], in1=v[:, cols], op=ALU.mult)
+            nc.vector.tensor_tensor(out=numer[:, cols], in0=numer[:, cols], in1=w[:, cols], op=ALU.mult)
+            nc.sync.dma_start(
+                out=out[:, first_e:last_e, :].rearrange("b e h -> b (e h)"), in_=numer[:, cols]
+            )
+
+        for u in range(UNITS):
+            e, c = divmod(u, CHUNKS)
+            piece = u // W_UNITS
+            if u % W_UNITS == 0 and piece + 2 < W_PIECES:
+                load_w(piece + 2)
+            if u % W_UNITS == 0 and piece + 1 < W_PIECES:
+                quantise_w(piece + 1)
+            if c == 0:
+                acc = acc_pool.tile([P, H1], F32, name="acc")
+
+            turned = [turned_pool.tile([P, PACK, B], F32, name="turned") for g in range(CHUNK_PASSES)]
+
+            def add_turned(term, opens, closes):
+                for g in range(CHUNK_PASSES):
+                    for t in range(PACK):
+                        nc.tensor.matmul(
+                            out=turned[g][:, t, :], lhsT=term[:, t, g * P : (g + 1) * P], rhs=ident[:],
+                            is_transpose=True,
+                            start=(opens and t == 0), stop=(closes and t == PACK - 1),
+                        )
+
+            for q in range(PAIRS):
+                even, odd = 2 * q, 2 * q + 1
+                tok_even = tok[c][:, even, :].rearrange("p (w t) -> p t w", t=PACK)
+                tok_odd = tok[c][:, odd, :].rearrange("p (w t) -> p t w", t=PACK)
+                split = q == PAIRS - 1 and c % 2 == 1
+                term = term_pool.tile([P, PACK, CHUNK // PACK], F32, name="term")
+                nc.scalar.activation(
+                    out=term[:], in_=tok_even, func=ACT.Copy, scale=disp[:, e, even : even + 1]
+                )
+                if split:
+                    add_turned(term, False, False)
+                    term = term_pool.tile([P, PACK, CHUNK // PACK], F32, name="term")
+                    nc.vector.tensor_scalar_mul(
+                        out=term[:], in0=tok_odd, scalar1=disp[:, e, odd : odd + 1]
+                    )
+                else:
+                    nc.vector.scalar_tensor_tensor(
+                        out=term[:], in0=tok_odd, scalar=disp[:, e, odd : odd + 1], in1=term[:],
+                        op0=ALU.mult, op1=ALU.add,
+                    )
+                add_turned(term, q == 0, q == PAIRS - 1)
+
+            if u == UNITS - 1:
+                mish_and_store(0, E - 1)
+
+            grouped = slot_pool.tile([P, CHUNK_PASSES, B, PACK], BF16, name="grouped", align_bytes=64)
+            for g in range(CHUNK_PASSES):
+                nc.scalar.copy(out=grouped[:, g, :, :], in_=turned[g][:].rearrange("p t b -> p b t"))
+            s_codes = slot_pool.tile([P, CHUNK_PASSES * B], U32, name="s_codes", align_bytes=64)
+            s_scales = slot_pool.tile([P, CHUNK_PASSES * B], U8, name="s_scales", align_bytes=64)
+            nc.vector.quantize_mx(
+                out=s_codes[:].bitcast(FP8X4),
+                scales=s_scales[:],
+                in_=grouped[:].rearrange("p g b t -> p (g b t)"),
+            )
+            for g in range(CHUNK_PASSES):
+                w_cols = slice(((u % W_UNITS) * CHUNK_PASSES + g) * H1, ((u % W_UNITS) * CHUNK_PASSES + g + 1) * H1)
+                nc.tensor.matmul_mx(
+                    out=acc[:],
+                    lhsT=s_codes[:, g * B : (g + 1) * B].bitcast(FP8X4),
+                    lhsT_scale=s_scales[:, g * B : (g + 1) * B],
+                    rhs=w_codes[piece][:, w_cols].bitcast(FP8X4),
+                    rhs_scale=w_scales[piece][:, w_cols],
+                    start=(c == 0 and g == 0),
+                    stop=(c == CHUNKS - 1 and g == CHUNK_PASSES - 1),
+                )
+            if c == CHUNKS - 1:
+                layer_norm(e, acc)
+        mish_and_store(E - 1, E)

@@ -25,6 +25,10 @@ W_UNITS = 2
 W_PASSES = W_UNITS * CHUNK_PASSES
 W_PIECES = UNITS // W_UNITS
 PAIRS = N // 2
+PLAIN_B = P // N
+PLAIN_J = B // PLAIN_B
+PASSES = D // K_PASS
+PLAIN_HALF_FROM = E // 2
 MISH_CLAMP = 20.0
 
 FLOPS = 2 * E * B * D * H1 + 2 * B * N * E * D
@@ -40,17 +44,20 @@ def tile_softmoedynamics_pa_k_kernel(tc, tokens, logits, W1, b1, g1, be1, out):
         w_mx_pool = ctx.enter_context(tc.tile_pool(name="w_mx", bufs=3))
         term_pool = ctx.enter_context(tc.tile_pool(name="term", bufs=8))
         slot_pool = ctx.enter_context(tc.tile_pool(name="slot", bufs=3))
+        plain_pool = ctx.enter_context(tc.tile_pool(name="plain", bufs=2))
+        plain_raw_pool = ctx.enter_context(tc.tile_pool(name="plain_raw", bufs=4))
+        plain_keep = ctx.enter_context(tc.tile_pool(name="plain_keep", bufs=1))
         epi_pool = ctx.enter_context(tc.tile_pool(name="epi", bufs=2))
-        mish_pool = ctx.enter_context(tc.tile_pool(name="mish", bufs=1))
         turned_pool = ctx.enter_context(tc.psum_pool(name="turned", bufs=7))
         acc_pool = ctx.enter_context(tc.psum_pool(name="acc", bufs=1))
 
-        tok = [tok_pool.tile([P, N, CHUNK], BF16, name="tok%d" % c) for c in range(CHUNKS)]
+        widths = [CHUNK] * (CHUNKS - 1) + [CHUNK - K_PASS]
+        tok = [tok_pool.tile([P, N, widths[c]], BF16, name="tok%d" % c) for c in range(CHUNKS)]
 
         def load_tokens(c, q):
             agents = slice(2 * q, 2 * q + 2)
             nc.sync.dma_start(
-                out=tok[c][:, agents, :], in_=tokens[:, agents, c * CHUNK : (c + 1) * CHUNK]
+                out=tok[c][:, agents, :], in_=tokens[:, agents, c * CHUNK : c * CHUNK + widths[c]]
             )
 
         w_raw = {}
@@ -93,7 +100,6 @@ def tile_softmoedynamics_pa_k_kernel(tc, tokens, logits, W1, b1, g1, be1, out):
         for c in range(2, CHUNKS):
             for q in range(PAIRS):
                 load_tokens(c, q)
-
         bias_bc = const.tile([P, E * H1], BF16)
         gain_bc = const.tile([P, E * H1], BF16)
         shift_bc = const.tile([P, E * H1], BF16)
@@ -109,22 +115,87 @@ def tile_softmoedynamics_pa_k_kernel(tc, tokens, logits, W1, b1, g1, be1, out):
         warm = const.tile([P, 1], F32)
         nc.scalar.activation(out=warm[:], in_=minus_half[:], func=ACT.Exp)
 
-        lg_en = lg[:].rearrange("p n e -> p e n")
         top = const.tile([P, E], F32)
-        nc.vector.tensor_reduce(out=top[:], in_=lg_en, axis=AXIS.X, op=ALU.max)
-        disp = const.tile([P, E, N], F32)
+        nc.vector.tensor_reduce(out=top[:], in_=lg[:].rearrange("p n e -> p e n"), axis=AXIS.X, op=ALU.max)
+        disp = const.tile([P, N, E], F32)
         nc.vector.tensor_tensor(
-            out=disp[:], in0=lg_en, in1=top[:].unsqueeze(2).to_broadcast([P, E, N]), op=ALU.subtract
+            out=disp[:], in0=lg[:], in1=top[:].unsqueeze(1).to_broadcast([P, N, E]), op=ALU.subtract
         )
         nc.scalar.activation(out=disp[:], in_=disp[:], func=ACT.Exp)
         total = const.tile([P, E], F32)
-        nc.vector.tensor_reduce(out=total[:], in_=disp[:], axis=AXIS.X, op=ALU.add)
+        nc.vector.tensor_reduce(
+            out=total[:], in_=disp[:].rearrange("p n e -> p e n"), axis=AXIS.X, op=ALU.add
+        )
         nc.vector.reciprocal(out=total[:], in_=total[:])
         nc.vector.tensor_tensor(
-            out=disp[:], in0=disp[:], in1=total[:].unsqueeze(2).to_broadcast([P, E, N]), op=ALU.mult
+            out=disp[:], in0=disp[:], in1=total[:].unsqueeze(1).to_broadcast([P, N, E]), op=ALU.mult
         )
 
         quantise_w(0)
+
+        parked = out.rearrange("b e h -> (b e h)")[0 : B * N * E]
+        nc.gpsimd.dma_start(
+            out=parked.rearrange("(b x) -> b x", x=N * E), in_=disp[:].rearrange("p n e -> p (n e)")
+        )
+        disp_rows = const.tile([P, PLAIN_J, E], F32)
+        nc.gpsimd.dma_start(out=disp_rows[:], in_=parked.rearrange("(j p e) -> p j e", p=P, e=E))
+        own = const.tile([P, PLAIN_B], F32)
+        nc.vector.tensor_reduce(
+            out=own[:], in_=ident[:].rearrange("p (b n) -> p b n", n=N), axis=AXIS.X, op=ALU.add
+        )
+        diag = const.tile([P, PLAIN_J * E, PLAIN_B], F32)
+        nc.vector.tensor_tensor(
+            out=diag[:],
+            in0=disp_rows[:].rearrange("p j e -> p (j e)").unsqueeze(2).to_broadcast([P, PLAIN_J * E, PLAIN_B]),
+            in1=own[:].unsqueeze(1).to_broadcast([P, PLAIN_J * E, PLAIN_B]),
+            op=ALU.mult,
+        )
+
+        plain_steps = [(PASSES - 1, 0, j) for j in range(PLAIN_J)]
+        plain_steps += [(PASSES - 2, PLAIN_HALF_FROM, j) for j in range(PLAIN_J)]
+        plain_raw = {}
+        plain_grouped = {}
+        plain_codes = {}
+        plain_scales = {}
+
+        def load_plain(step):
+            k_pass, first_e, j = plain_steps[step]
+            raw = plain_raw_pool.tile([P, K_PASS], BF16, name="plain_raw")
+            rows = tokens.rearrange("(j b) n d -> j (b n) d", b=PLAIN_B)[j]
+            nc.sync.dma_start(out=raw[:], in_=rows[:, k_pass * K_PASS : (k_pass + 1) * K_PASS])
+            plain_raw[step] = raw
+
+        def plain_step(step):
+            k_pass, first_e, j = plain_steps[step]
+            experts = E - first_e
+            if step + 3 < len(plain_steps):
+                load_plain(step + 3)
+            words = plain_pool.tile([P, PACK, P], F32, name="words")
+            nc.vector.tensor_copy(out=words[:], in_=plain_raw[step][:].rearrange("p (w t) -> p t w", t=PACK))
+            if j == 0:
+                plain_grouped[k_pass] = plain_keep.tile([P, experts, B, PACK], BF16, name="plain_grouped", align_bytes=64)
+            grouped = plain_grouped[k_pass]
+            turned = turned_pool.tile([P, PACK, B], F32, name="turned")
+            for t in range(PACK):
+                nc.tensor.matmul(
+                    out=turned[:, t, : experts * PLAIN_B],
+                    lhsT=words[:, t, :],
+                    rhs=diag[:, j * E + first_e : (j + 1) * E, :].rearrange("p e b -> p (e b)"),
+                    start=True,
+                    stop=True,
+                )
+            nc.scalar.copy(
+                out=grouped[:, :, j * PLAIN_B : (j + 1) * PLAIN_B, :],
+                in_=turned[:, :, : experts * PLAIN_B].rearrange("p t (e b) -> p e b t", b=PLAIN_B),
+            )
+            if j == PLAIN_J - 1:
+                codes = plain_keep.tile([P, experts * B], U32, name="plain_codes%d" % k_pass, align_bytes=64)
+                scales = plain_keep.tile([P, experts * B], U8, name="plain_scales%d" % k_pass, align_bytes=64)
+                nc.vector.quantize_mx(
+                    out=codes[:].bitcast(FP8X4), scales=scales[:], in_=grouped[:].rearrange("p e b t -> p (e b t)")
+                )
+                plain_codes[k_pass] = codes
+                plain_scales[k_pass] = scales
 
         v = const.tile([P, E * H1], F32)
 
@@ -149,11 +220,12 @@ def tile_softmoedynamics_pa_k_kernel(tc, tokens, logits, W1, b1, g1, be1, out):
                 op0=ALU.mult, op1=ALU.add,
             )
 
-        w = mish_pool.tile([P, E * H1], F32)
-        numer = mish_pool.tile([P, E * H1], F32)
-
         def mish_and_store(first_e, last_e):
             cols = slice(first_e * H1, last_e * H1)
+            w_tile = term_pool.tile([P, PACK, CHUNK // PACK], F32, name="term")
+            numer_tile = term_pool.tile([P, PACK, CHUNK // PACK], F32, name="term")
+            w = w_tile[:].rearrange("p t w -> p (t w)")
+            numer = numer_tile[:].rearrange("p t w -> p (t w)")
             nc.vector.tensor_scalar_min(out=w[:, cols], in0=v[:, cols], scalar1=MISH_CLAMP)
             nc.scalar.activation(out=w[:, cols], in_=w[:, cols], func=ACT.Exp)
             nc.vector.scalar_tensor_tensor(
@@ -167,6 +239,9 @@ def tile_softmoedynamics_pa_k_kernel(tc, tokens, logits, W1, b1, g1, be1, out):
                 out=out[:, first_e:last_e, :].rearrange("b e h -> b (e h)"), in_=numer[:, cols]
             )
 
+        for step in range(3):
+            load_plain(step)
+        next_step = 0
         for u in range(UNITS):
             e, c = divmod(u, CHUNKS)
             piece = u // W_UNITS
@@ -176,11 +251,35 @@ def tile_softmoedynamics_pa_k_kernel(tc, tokens, logits, W1, b1, g1, be1, out):
                 quantise_w(piece + 1)
             if c == 0:
                 acc = acc_pool.tile([P, H1], F32, name="acc")
+            steps = 2 if e < 2 and 2 <= c < 6 else 0
 
-            turned = [turned_pool.tile([P, PACK, B], F32, name="turned") for g in range(CHUNK_PASSES)]
+            def multiply(k_pass, codes, scales, cols, opens=False, closes=False):
+                w_pass = k_pass % W_PASSES
+                nc.tensor.matmul_mx(
+                    out=acc[:],
+                    lhsT=codes[:, cols].bitcast(FP8X4),
+                    lhsT_scale=scales[:, cols],
+                    rhs=w_codes[piece][:, w_pass * H1 : (w_pass + 1) * H1].bitcast(FP8X4),
+                    rhs_scale=w_scales[piece][:, w_pass * H1 : (w_pass + 1) * H1],
+                    start=opens,
+                    stop=closes,
+                )
+
+            def multiply_plain(k_pass, first_e):
+                cols = slice((e - first_e) * B, (e - first_e + 1) * B)
+                multiply(k_pass, plain_codes[k_pass], plain_scales[k_pass], cols)
+
+            half = e < PLAIN_HALF_FROM
+            if c == CHUNKS - 1 and not half:
+                continue
+            last = c == (CHUNKS - 1 if half else CHUNKS - 2)
+            width = widths[c]
+            passes = width // K_PASS
+
+            turned = [turned_pool.tile([P, PACK, B], F32, name="turned") for g in range(passes)]
 
             def add_turned(term, opens, closes):
-                for g in range(CHUNK_PASSES):
+                for g in range(passes):
                     for t in range(PACK):
                         nc.tensor.matmul(
                             out=turned[g][:, t, :], lhsT=term[:, t, g * P : (g + 1) * P], rhs=ident[:],
@@ -194,46 +293,48 @@ def tile_softmoedynamics_pa_k_kernel(tc, tokens, logits, W1, b1, g1, be1, out):
                 tok_odd = tok[c][:, odd, :].rearrange("p (w t) -> p t w", t=PACK)
                 split = q == PAIRS - 1 and c % 2 == 1
                 term = term_pool.tile([P, PACK, CHUNK // PACK], F32, name="term")
+                made = term[:, :, : width // PACK]
                 nc.scalar.activation(
-                    out=term[:], in_=tok_even, func=ACT.Copy, scale=disp[:, e, even : even + 1]
+                    out=made, in_=tok_even, func=ACT.Copy, scale=disp[:, even, e : e + 1]
                 )
                 if split:
                     add_turned(term, False, False)
                     term = term_pool.tile([P, PACK, CHUNK // PACK], F32, name="term")
                     nc.vector.tensor_scalar_mul(
-                        out=term[:], in0=tok_odd, scalar1=disp[:, e, odd : odd + 1]
+                        out=term[:, :, : width // PACK], in0=tok_odd, scalar1=disp[:, odd, e : e + 1]
                     )
                 else:
                     nc.vector.scalar_tensor_tensor(
-                        out=term[:], in0=tok_odd, scalar=disp[:, e, odd : odd + 1], in1=term[:],
+                        out=made, in0=tok_odd, scalar=disp[:, odd, e : e + 1], in1=made,
                         op0=ALU.mult, op1=ALU.add,
                     )
                 add_turned(term, q == 0, q == PAIRS - 1)
 
-            if u == UNITS - 1:
+            if last and e == E - 1:
                 mish_and_store(0, E - 1)
 
             grouped = slot_pool.tile([P, CHUNK_PASSES, B, PACK], BF16, name="grouped", align_bytes=64)
-            for g in range(CHUNK_PASSES):
+            for g in range(passes):
                 nc.scalar.copy(out=grouped[:, g, :, :], in_=turned[g][:].rearrange("p t b -> p b t"))
             s_codes = slot_pool.tile([P, CHUNK_PASSES * B], U32, name="s_codes", align_bytes=64)
             s_scales = slot_pool.tile([P, CHUNK_PASSES * B], U8, name="s_scales", align_bytes=64)
             nc.vector.quantize_mx(
-                out=s_codes[:].bitcast(FP8X4),
-                scales=s_scales[:],
-                in_=grouped[:].rearrange("p g b t -> p (g b t)"),
+                out=s_codes[:, : passes * B].bitcast(FP8X4),
+                scales=s_scales[:, : passes * B],
+                in_=grouped[:, :passes, :, :].rearrange("p g b t -> p (g b t)"),
             )
-            for g in range(CHUNK_PASSES):
-                w_cols = slice(((u % W_UNITS) * CHUNK_PASSES + g) * H1, ((u % W_UNITS) * CHUNK_PASSES + g + 1) * H1)
-                nc.tensor.matmul_mx(
-                    out=acc[:],
-                    lhsT=s_codes[:, g * B : (g + 1) * B].bitcast(FP8X4),
-                    lhsT_scale=s_scales[:, g * B : (g + 1) * B],
-                    rhs=w_codes[piece][:, w_cols].bitcast(FP8X4),
-                    rhs_scale=w_scales[piece][:, w_cols],
-                    start=(c == 0 and g == 0),
-                    stop=(c == CHUNKS - 1 and g == CHUNK_PASSES - 1),
+            if last:
+                multiply_plain(PASSES - 1, 0)
+                if not half:
+                    multiply_plain(PASSES - 2, PLAIN_HALF_FROM)
+            for g in range(passes):
+                multiply(
+                    c * CHUNK_PASSES + g, s_codes, s_scales, slice(g * B, (g + 1) * B),
+                    opens=(c == 0 and g == 0), closes=(last and g == passes - 1),
                 )
-            if c == CHUNKS - 1:
+            if last:
                 layer_norm(e, acc)
+            for step in range(next_step, next_step + steps):
+                plain_step(step)
+            next_step += steps
         mish_and_store(E - 1, E)

@@ -25,6 +25,7 @@ W_UNITS = 2
 W_PASSES = W_UNITS * CHUNK_PASSES
 W_PIECES = UNITS // W_UNITS
 PAIRS = N // 2
+RUN = 8
 PLAIN_B = P // N
 PLAIN_J = B // PLAIN_B
 PASSES = D // K_PASS
@@ -144,12 +145,14 @@ def tile_softmoedynamics_pa_k_kernel(tc, tokens, logits, W1, b1, g1, be1, out):
             out=own[:], in_=ident[:].rearrange("p (b n) -> p b n", n=N), axis=AXIS.X, op=ALU.add
         )
         diag = const.tile([P, PLAIN_J * E, PLAIN_B], F32)
-        nc.vector.tensor_tensor(
-            out=diag[:],
-            in0=disp_rows[:].rearrange("p j e -> p (j e)").unsqueeze(2).to_broadcast([P, PLAIN_J * E, PLAIN_B]),
-            in1=own[:].unsqueeze(1).to_broadcast([P, PLAIN_J * E, PLAIN_B]),
-            op=ALU.mult,
-        )
+
+        def make_diag():
+            nc.vector.tensor_tensor(
+                out=diag[:],
+                in0=disp_rows[:].rearrange("p j e -> p (j e)").unsqueeze(2).to_broadcast([P, PLAIN_J * E, PLAIN_B]),
+                in1=own[:].unsqueeze(1).to_broadcast([P, PLAIN_J * E, PLAIN_B]),
+                op=ALU.mult,
+            )
 
         plain_steps = [(PASSES - 1, 0, j) for j in range(PLAIN_J)]
         plain_steps += [(PASSES - 2, PLAIN_HALF_FROM, j) for j in range(PLAIN_J)]
@@ -251,7 +254,7 @@ def tile_softmoedynamics_pa_k_kernel(tc, tokens, logits, W1, b1, g1, be1, out):
                 quantise_w(piece + 1)
             if c == 0:
                 acc = acc_pool.tile([P, H1], F32, name="acc")
-            steps = 2 if e < 2 and 2 <= c < 6 else 0
+            steps = 2 if e < 2 and 3 <= c < 7 else 0
 
             def multiply(k_pass, codes, scales, cols, opens=False, closes=False):
                 w_pass = k_pass % W_PASSES
@@ -289,13 +292,13 @@ def tile_softmoedynamics_pa_k_kernel(tc, tokens, logits, W1, b1, g1, be1, out):
 
             for q in range(PAIRS):
                 even, odd = 2 * q, 2 * q + 1
-                tok_even = tok[c][:, even, :].rearrange("p (w t) -> p t w", t=PACK)
+                tok_even = tok[c][:, even, :].rearrange("p (w i t) -> p w t i", i=RUN, t=PACK)
                 tok_odd = tok[c][:, odd, :].rearrange("p (w t) -> p t w", t=PACK)
                 split = q == PAIRS - 1 and c % 2 == 1
                 term = term_pool.tile([P, PACK, CHUNK // PACK], F32, name="term")
                 made = term[:, :, : width // PACK]
                 nc.scalar.activation(
-                    out=made, in_=tok_even, func=ACT.Copy, scale=disp[:, even, e : e + 1]
+                    out=made.rearrange("p t (w i) -> p w t i", i=RUN), in_=tok_even, func=ACT.Copy, scale=disp[:, even, e : e + 1]
                 )
                 if split:
                     add_turned(term, False, False)
@@ -334,6 +337,8 @@ def tile_softmoedynamics_pa_k_kernel(tc, tokens, logits, W1, b1, g1, be1, out):
                 )
             if last:
                 layer_norm(e, acc)
+            if u == 3:
+                make_diag()
             for step in range(next_step, next_step + steps):
                 plain_step(step)
             next_step += steps

@@ -25,7 +25,6 @@ W_UNITS = 2
 W_PASSES = W_UNITS * CHUNK_PASSES
 W_PIECES = UNITS // W_UNITS
 PAIRS = N // 2
-RUN = 8
 PLAIN_B = P // N
 PLAIN_J = B // PLAIN_B
 PASSES = D // K_PASS
@@ -147,7 +146,7 @@ def tile_softmoedynamics_pa_k_kernel(tc, tokens, logits, W1, b1, g1, be1, out):
         diag = const.tile([P, PLAIN_J * E, PLAIN_B], F32)
 
         def make_diag():
-            nc.vector.tensor_tensor(
+            nc.gpsimd.tensor_tensor(
                 out=diag[:],
                 in0=disp_rows[:].rearrange("p j e -> p (j e)").unsqueeze(2).to_broadcast([P, PLAIN_J * E, PLAIN_B]),
                 in1=own[:].unsqueeze(1).to_broadcast([P, PLAIN_J * E, PLAIN_B]),
@@ -225,10 +224,8 @@ def tile_softmoedynamics_pa_k_kernel(tc, tokens, logits, W1, b1, g1, be1, out):
 
         def mish_and_store(first_e, last_e):
             cols = slice(first_e * H1, last_e * H1)
-            w_tile = term_pool.tile([P, PACK, CHUNK // PACK], F32, name="term")
-            numer_tile = term_pool.tile([P, PACK, CHUNK // PACK], F32, name="term")
-            w = w_tile[:].rearrange("p t w -> p (t w)")
-            numer = numer_tile[:].rearrange("p t w -> p (t w)")
+            w = term_pool.tile([P, CHUNK], F32, name="term")
+            numer = term_pool.tile([P, CHUNK], F32, name="term")
             nc.vector.tensor_scalar_min(out=w[:, cols], in0=v[:, cols], scalar1=MISH_CLAMP)
             nc.scalar.activation(out=w[:, cols], in_=w[:, cols], func=ACT.Exp)
             nc.vector.scalar_tensor_tensor(
@@ -285,26 +282,26 @@ def tile_softmoedynamics_pa_k_kernel(tc, tokens, logits, W1, b1, g1, be1, out):
                 for g in range(passes):
                     for t in range(PACK):
                         nc.tensor.matmul(
-                            out=turned[g][:, t, :], lhsT=term[:, t, g * P : (g + 1) * P], rhs=ident[:],
+                            out=turned[g][:, t, :], lhsT=term[:, g * K_PASS + t : (g + 1) * K_PASS : PACK], rhs=ident[:],
                             is_transpose=True,
                             start=(opens and t == 0), stop=(closes and t == PACK - 1),
                         )
 
             for q in range(PAIRS):
                 even, odd = 2 * q, 2 * q + 1
-                tok_even = tok[c][:, even, :].rearrange("p (w i t) -> p w t i", i=RUN, t=PACK)
-                tok_odd = tok[c][:, odd, :].rearrange("p (w t) -> p t w", t=PACK)
+                tok_even = tok[c][:, even, :]
+                tok_odd = tok[c][:, odd, :]
                 split = q == PAIRS - 1 and c % 2 == 1
-                term = term_pool.tile([P, PACK, CHUNK // PACK], F32, name="term")
-                made = term[:, :, : width // PACK]
+                term = term_pool.tile([P, CHUNK], F32, name="term")
+                made = term[:, :width]
                 nc.scalar.activation(
-                    out=made.rearrange("p t (w i) -> p w t i", i=RUN), in_=tok_even, func=ACT.Copy, scale=disp[:, even, e : e + 1]
+                    out=made, in_=tok_even, func=ACT.Copy, scale=disp[:, even, e : e + 1]
                 )
                 if split:
                     add_turned(term, False, False)
-                    term = term_pool.tile([P, PACK, CHUNK // PACK], F32, name="term")
+                    term = term_pool.tile([P, CHUNK], F32, name="term")
                     nc.vector.tensor_scalar_mul(
-                        out=term[:, :, : width // PACK], in0=tok_odd, scalar1=disp[:, odd, e : e + 1]
+                        out=term[:, :width], in0=tok_odd, scalar1=disp[:, odd, e : e + 1]
                     )
                 else:
                     nc.vector.scalar_tensor_tensor(

@@ -291,23 +291,15 @@ def tile_softmoedynamics_pa_k_kernel(tc, tokens, logits, W1, b1, g1, be1, out):
                 even, odd = 2 * q, 2 * q + 1
                 tok_even = tok[c][:, even, :]
                 tok_odd = tok[c][:, odd, :]
-                split = q == PAIRS - 1 and c % 2 == 1
                 term = term_pool.tile([P, CHUNK], F32, name="term")
                 made = term[:, :width]
                 nc.scalar.activation(
                     out=made, in_=tok_even, func=ACT.Copy, scale=disp[:, even, e : e + 1]
                 )
-                if split:
-                    add_turned(term, False, False)
-                    term = term_pool.tile([P, CHUNK], F32, name="term")
-                    nc.vector.tensor_scalar_mul(
-                        out=term[:, :width], in0=tok_odd, scalar1=disp[:, odd, e : e + 1]
-                    )
-                else:
-                    nc.vector.scalar_tensor_tensor(
-                        out=made, in0=tok_odd, scalar=disp[:, odd, e : e + 1], in1=made,
-                        op0=ALU.mult, op1=ALU.add,
-                    )
+                nc.vector.scalar_tensor_tensor(
+                    out=made, in0=tok_odd, scalar=disp[:, odd, e : e + 1], in1=made,
+                    op0=ALU.mult, op1=ALU.add,
+                )
                 add_turned(term, q == 0, q == PAIRS - 1)
 
             if last and e == E - 1:

@@ -42,12 +42,13 @@ def tile_softmoedynamics_pa_k_kernel(tc, tokens, logits, W1, b1, g1, be1, out):
         w_raw_pool = ctx.enter_context(tc.tile_pool(name="w_raw", bufs=3))
         w_grp_pool = ctx.enter_context(tc.tile_pool(name="w_grp", bufs=2))
         w_mx_pool = ctx.enter_context(tc.tile_pool(name="w_mx", bufs=3))
-        term_pool = ctx.enter_context(tc.tile_pool(name="term", bufs=8))
+        term_pool = ctx.enter_context(tc.tile_pool(name="term", bufs=7))
         slot_pool = ctx.enter_context(tc.tile_pool(name="slot", bufs=3))
         plain_pool = ctx.enter_context(tc.tile_pool(name="plain", bufs=2))
         plain_raw_pool = ctx.enter_context(tc.tile_pool(name="plain_raw", bufs=4))
         plain_keep = ctx.enter_context(tc.tile_pool(name="plain_keep", bufs=1))
         epi_pool = ctx.enter_context(tc.tile_pool(name="epi", bufs=2))
+        mish_pool = ctx.enter_context(tc.tile_pool(name="mish", bufs=1))
         turned_pool = ctx.enter_context(tc.psum_pool(name="turned", bufs=7))
         acc_pool = ctx.enter_context(tc.psum_pool(name="acc", bufs=1))
 
@@ -61,6 +62,7 @@ def tile_softmoedynamics_pa_k_kernel(tc, tokens, logits, W1, b1, g1, be1, out):
             )
 
         w_raw = {}
+        w_grouped = {}
         w_codes = {}
         w_scales = {}
 
@@ -75,31 +77,30 @@ def tile_softmoedynamics_pa_k_kernel(tc, tokens, logits, W1, b1, g1, be1, out):
                 )
             w_raw[piece] = raw
 
-        def quantise_w(piece):
+        def regroup_w(piece):
             grouped = w_grp_pool.tile([P, W_PASSES * H1, PACK], BF16, name="w_grp", align_bytes=64)
             nc.vector.tensor_copy(
                 out=grouped[:].rearrange("p (c i) t -> p c t i", i=4),
                 in_=w_raw[piece][:].rearrange("p t (c i) -> p c t i", i=4),
             )
+            w_grouped[piece] = grouped
+
+        def quantise_w(piece):
             w_codes[piece] = w_mx_pool.tile([P, W_PASSES * H1], U32, name="w_codes", align_bytes=64)
             w_scales[piece] = w_mx_pool.tile([P, W_PASSES * H1], U8, name="w_scales", align_bytes=64)
             nc.vector.quantize_mx(
                 out=w_codes[piece][:].bitcast(FP8X4),
                 scales=w_scales[piece][:],
-                in_=grouped[:].rearrange("p w t -> p (w t)"),
+                in_=w_grouped[piece][:].rearrange("p w t -> p (w t)"),
             )
 
         lg = const.tile([P, N, E], BF16)
         nc.sync.dma_start(out=lg[:], in_=logits)
-        for q in range(PAIRS):
-            load_tokens(0, q)
-        load_w(0)
-        for q in range(PAIRS):
-            load_tokens(1, q)
-        load_w(1)
-        for c in range(2, CHUNKS):
+        for c in range(CHUNKS):
             for q in range(PAIRS):
                 load_tokens(c, q)
+            if c % W_UNITS == 0 and c // W_UNITS < 3:
+                load_w(c // W_UNITS)
         bias_bc = const.tile([P, E * H1], BF16)
         gain_bc = const.tile([P, E * H1], BF16)
         shift_bc = const.tile([P, E * H1], BF16)
@@ -131,6 +132,7 @@ def tile_softmoedynamics_pa_k_kernel(tc, tokens, logits, W1, b1, g1, be1, out):
             out=disp[:], in0=disp[:], in1=total[:].unsqueeze(1).to_broadcast([P, N, E]), op=ALU.mult
         )
 
+        regroup_w(0)
         quantise_w(0)
 
         parked = out.rearrange("b e h -> (b e h)")[0 : B * N * E]
@@ -156,6 +158,8 @@ def tile_softmoedynamics_pa_k_kernel(tc, tokens, logits, W1, b1, g1, be1, out):
         plain_steps = [(PASSES - 1, 0, j) for j in range(PLAIN_J)]
         plain_steps += [(PASSES - 2, PLAIN_HALF_FROM, j) for j in range(PLAIN_J)]
         plain_raw = {}
+        plain_words = {}
+        plain_turned = {}
         plain_grouped = {}
         plain_codes = {}
         plain_scales = {}
@@ -167,168 +171,269 @@ def tile_softmoedynamics_pa_k_kernel(tc, tokens, logits, W1, b1, g1, be1, out):
             nc.sync.dma_start(out=raw[:], in_=rows[:, k_pass * K_PASS : (k_pass + 1) * K_PASS])
             plain_raw[step] = raw
 
-        def plain_step(step):
-            k_pass, first_e, j = plain_steps[step]
-            experts = E - first_e
-            if step + 3 < len(plain_steps):
-                load_plain(step + 3)
+        def plain_cast(step):
             words = plain_pool.tile([P, PACK, P], F32, name="words")
             nc.vector.tensor_copy(out=words[:], in_=plain_raw[step][:].rearrange("p (w t) -> p t w", t=PACK))
-            if j == 0:
-                plain_grouped[k_pass] = plain_keep.tile([P, experts, B, PACK], BF16, name="plain_grouped", align_bytes=64)
-            grouped = plain_grouped[k_pass]
+            plain_words[step] = words
+            if step + 3 < len(plain_steps):
+                load_plain(step + 3)
+
+        def plain_multiply(step):
+            k_pass, first_e, j = plain_steps[step]
             turned = turned_pool.tile([P, PACK, B], F32, name="turned")
             for t in range(PACK):
                 nc.tensor.matmul(
-                    out=turned[:, t, : experts * PLAIN_B],
-                    lhsT=words[:, t, :],
+                    out=turned[:, t, : (E - first_e) * PLAIN_B],
+                    lhsT=plain_words[step][:, t, :],
                     rhs=diag[:, j * E + first_e : (j + 1) * E, :].rearrange("p e b -> p (e b)"),
                     start=True,
                     stop=True,
                 )
+            plain_turned[step] = turned
+
+        def plain_copy(step):
+            k_pass, first_e, j = plain_steps[step]
+            experts = E - first_e
+            if j == 0:
+                plain_grouped[k_pass] = plain_keep.tile([P, experts, B, PACK], BF16, name="plain_grouped", align_bytes=64)
             nc.scalar.copy(
-                out=grouped[:, :, j * PLAIN_B : (j + 1) * PLAIN_B, :],
-                in_=turned[:, :, : experts * PLAIN_B].rearrange("p t (e b) -> p e b t", b=PLAIN_B),
+                out=plain_grouped[k_pass][:, :, j * PLAIN_B : (j + 1) * PLAIN_B, :],
+                in_=plain_turned[step][:, :, : experts * PLAIN_B].rearrange("p t (e b) -> p e b t", b=PLAIN_B),
             )
-            if j == PLAIN_J - 1:
-                codes = plain_keep.tile([P, experts * B], U32, name="plain_codes%d" % k_pass, align_bytes=64)
-                scales = plain_keep.tile([P, experts * B], U8, name="plain_scales%d" % k_pass, align_bytes=64)
-                nc.vector.quantize_mx(
-                    out=codes[:].bitcast(FP8X4), scales=scales[:], in_=grouped[:].rearrange("p e b t -> p (e b t)")
-                )
-                plain_codes[k_pass] = codes
-                plain_scales[k_pass] = scales
+
+        def plain_quantise(k_pass, first_e):
+            experts = E - first_e
+            codes = plain_keep.tile([P, experts * B], U32, name="plain_codes%d" % k_pass, align_bytes=64)
+            scales = plain_keep.tile([P, experts * B], U8, name="plain_scales%d" % k_pass, align_bytes=64)
+            nc.vector.quantize_mx(
+                out=codes[:].bitcast(FP8X4),
+                scales=scales[:],
+                in_=plain_grouped[k_pass][:].rearrange("p e b t -> p (e b t)"),
+            )
+            plain_codes[k_pass] = codes
+            plain_scales[k_pass] = scales
 
         v = const.tile([P, E * H1], F32)
 
-        def layer_norm(e, acc):
+        acc = {}
+        mean_var = {}
+        rstd = {}
+
+        def norm_add(e):
             cols = slice(e * H1, (e + 1) * H1)
-            nc.vector.tensor_tensor(out=v[:, cols], in0=acc[:], in1=bias_bc[:, cols], op=ALU.add)
+            nc.vector.tensor_tensor(out=v[:, cols], in0=acc[e][:], in1=bias_bc[:, cols], op=ALU.add)
+
+        def norm_stats(e):
             stats = epi_pool.tile([P, 6], F32, name="stats")
-            nc.vector.bn_stats(out=stats[:], in_=v[:, cols])
-            mean_var = epi_pool.tile([P, 2], F32, name="mean_var")
-            nc.vector.bn_aggr(out=mean_var[:], in_=stats[:])
-            rstd = epi_pool.tile([P, 1], F32, name="rstd")
+            nc.vector.bn_stats(out=stats[:], in_=v[:, e * H1 : (e + 1) * H1])
+            mean_var[e] = epi_pool.tile([P, 2], F32, name="mean_var")
+            nc.vector.bn_aggr(out=mean_var[e][:], in_=stats[:])
+            rstd[e] = epi_pool.tile([P, 1], F32, name="rstd")
             nc.gpsimd.tensor_scalar(
-                out=rstd[:], in0=mean_var[:, 1:2], scalar1=EPS, scalar2=1.0, op0=ALU.add, op1=ALU.mult
+                out=rstd[e][:], in0=mean_var[e][:, 1:2], scalar1=EPS, scalar2=1.0, op0=ALU.add, op1=ALU.mult
             )
-            nc.gpsimd.tensor_tensor(out=rstd[:], in0=rstd[:], in1=minus_half[:], op=ALU.pow)
+            nc.gpsimd.tensor_tensor(out=rstd[e][:], in0=rstd[e][:], in1=minus_half[:], op=ALU.pow)
+
+        def norm_gain(e):
+            cols = slice(e * H1, (e + 1) * H1)
             nc.vector.scalar_tensor_tensor(
-                out=v[:, cols], in0=v[:, cols], scalar=mean_var[:, 0:1], in1=gain_bc[:, cols],
+                out=v[:, cols], in0=v[:, cols], scalar=mean_var[e][:, 0:1], in1=gain_bc[:, cols],
                 op0=ALU.subtract, op1=ALU.mult,
             )
+
+        def norm_shift(e):
+            cols = slice(e * H1, (e + 1) * H1)
             nc.vector.scalar_tensor_tensor(
-                out=v[:, cols], in0=v[:, cols], scalar=rstd[:], in1=shift_bc[:, cols],
+                out=v[:, cols], in0=v[:, cols], scalar=rstd[e][:], in1=shift_bc[:, cols],
                 op0=ALU.mult, op1=ALU.add,
             )
 
-        def mish_and_store(first_e, last_e):
-            cols = slice(first_e * H1, last_e * H1)
-            w = term_pool.tile([P, CHUNK], F32, name="term")
-            numer = term_pool.tile([P, CHUNK], F32, name="term")
-            nc.vector.tensor_scalar_min(out=w[:, cols], in0=v[:, cols], scalar1=MISH_CLAMP)
-            nc.scalar.activation(out=w[:, cols], in_=w[:, cols], func=ACT.Exp)
+        w_exp = mish_pool.tile([P, E * H1], F32)
+        numer = mish_pool.tile([P, E * H1], F32)
+
+        def mish_exp(cols):
+            nc.vector.tensor_scalar_min(out=w_exp[:, cols], in0=v[:, cols], scalar1=MISH_CLAMP)
+            nc.scalar.activation(out=w_exp[:, cols], in_=w_exp[:, cols], func=ACT.Exp)
+
+        def mish_numer(cols):
             nc.vector.scalar_tensor_tensor(
-                out=numer[:, cols], in0=w[:, cols], scalar=2.0, in1=w[:, cols], op0=ALU.add, op1=ALU.mult
+                out=numer[:, cols], in0=w_exp[:, cols], scalar=2.0, in1=w_exp[:, cols], op0=ALU.add, op1=ALU.mult
             )
-            nc.vector.tensor_scalar_add(out=w[:, cols], in0=numer[:, cols], scalar1=2.0)
-            nc.vector.reciprocal(out=w[:, cols], in_=w[:, cols])
+
+        def mish_denom(cols):
+            nc.vector.tensor_scalar_add(out=w_exp[:, cols], in0=numer[:, cols], scalar1=2.0)
+
+        def mish_times_v(cols):
             nc.vector.tensor_tensor(out=numer[:, cols], in0=numer[:, cols], in1=v[:, cols], op=ALU.mult)
-            nc.vector.tensor_tensor(out=numer[:, cols], in0=numer[:, cols], in1=w[:, cols], op=ALU.mult)
+
+        def mish_reciprocal(cols):
+            nc.vector.reciprocal(out=w_exp[:, cols], in_=w_exp[:, cols])
+
+        def mish_store(first_e, last_e):
+            cols = slice(first_e * H1, last_e * H1)
+            nc.vector.tensor_tensor(out=numer[:, cols], in0=numer[:, cols], in1=w_exp[:, cols], op=ALU.mult)
             nc.sync.dma_start(
                 out=out[:, first_e:last_e, :].rearrange("b e h -> b (e h)"), in_=numer[:, cols]
             )
 
-        for step in range(3):
-            load_plain(step)
-        next_step = 0
-        for u in range(UNITS):
-            e, c = divmod(u, CHUNKS)
-            piece = u // W_UNITS
-            if u % W_UNITS == 0 and piece + 2 < W_PIECES:
-                load_w(piece + 2)
-            if u % W_UNITS == 0 and piece + 1 < W_PIECES:
-                quantise_w(piece + 1)
-            if c == 0:
-                acc = acc_pool.tile([P, H1], F32, name="acc")
-            steps = 2 if e < 2 and 3 <= c < 7 else 0
+        turned = {}
+        slot_grouped = {}
+        slot_codes = {}
+        slot_scales = {}
 
-            def multiply(k_pass, codes, scales, cols, opens=False, closes=False):
-                w_pass = k_pass % W_PASSES
-                nc.tensor.matmul_mx(
-                    out=acc[:],
-                    lhsT=codes[:, cols].bitcast(FP8X4),
-                    lhsT_scale=scales[:, cols],
-                    rhs=w_codes[piece][:, w_pass * H1 : (w_pass + 1) * H1].bitcast(FP8X4),
-                    rhs_scale=w_scales[piece][:, w_pass * H1 : (w_pass + 1) * H1],
-                    start=opens,
-                    stop=closes,
-                )
-
-            def multiply_plain(k_pass, first_e):
-                cols = slice((e - first_e) * B, (e - first_e + 1) * B)
-                multiply(k_pass, plain_codes[k_pass], plain_scales[k_pass], cols)
-
-            half = e < PLAIN_HALF_FROM
-            if c == CHUNKS - 1 and not half:
-                continue
-            last = c == (CHUNKS - 1 if half else CHUNKS - 2)
-            width = widths[c]
-            passes = width // K_PASS
-
-            turned = [turned_pool.tile([P, PACK, B], F32, name="turned") for g in range(passes)]
-
-            def add_turned(term, opens, closes):
-                for g in range(passes):
-                    for t in range(PACK):
-                        nc.tensor.matmul(
-                            out=turned[g][:, t, :], lhsT=term[:, g * K_PASS + t : (g + 1) * K_PASS : PACK], rhs=ident[:],
-                            is_transpose=True,
-                            start=(opens and t == 0), stop=(closes and t == PACK - 1),
-                        )
-
-            for q in range(PAIRS):
-                even, odd = 2 * q, 2 * q + 1
-                tok_even = tok[c][:, even, :]
-                tok_odd = tok[c][:, odd, :]
-                term = term_pool.tile([P, CHUNK], F32, name="term")
-                made = term[:, :width]
-                nc.scalar.activation(
-                    out=made, in_=tok_even, func=ACT.Copy, scale=disp[:, even, e : e + 1]
-                )
-                nc.vector.scalar_tensor_tensor(
-                    out=made, in0=tok_odd, scalar=disp[:, odd, e : e + 1], in1=made,
-                    op0=ALU.mult, op1=ALU.add,
-                )
-                add_turned(term, q == 0, q == PAIRS - 1)
-
-            if last and e == E - 1:
-                mish_and_store(0, E - 1)
-
-            grouped = slot_pool.tile([P, CHUNK_PASSES, B, PACK], BF16, name="grouped", align_bytes=64)
-            for g in range(passes):
-                nc.scalar.copy(out=grouped[:, g, :, :], in_=turned[g][:].rearrange("p t b -> p b t"))
-            s_codes = slot_pool.tile([P, CHUNK_PASSES * B], U32, name="s_codes", align_bytes=64)
-            s_scales = slot_pool.tile([P, CHUNK_PASSES * B], U8, name="s_scales", align_bytes=64)
-            nc.vector.quantize_mx(
-                out=s_codes[:, : passes * B].bitcast(FP8X4),
-                scales=s_scales[:, : passes * B],
-                in_=grouped[:, :passes, :, :].rearrange("p g b t -> p (g b t)"),
+        def scale_even(e, c, q):
+            term = term_pool.tile([P, CHUNK], F32, name="term")
+            nc.scalar.activation(
+                out=term[:, : widths[c]], in_=tok[c][:, 2 * q, :], func=ACT.Copy, scale=disp[:, 2 * q, e : e + 1]
             )
+            return term
+
+        def add_odd(term, e, c, q):
+            made = term[:, : widths[c]]
+            nc.vector.scalar_tensor_tensor(
+                out=made, in0=tok[c][:, 2 * q + 1, :], scalar=disp[:, 2 * q + 1, e : e + 1], in1=made,
+                op0=ALU.mult, op1=ALU.add,
+            )
+
+        def transpose_term(term, e, c, q):
+            passes = widths[c] // K_PASS
+            if q == 0:
+                banks = [turned_pool.tile([P, PACK, B], F32, name="turned") for g in range(passes)]
+                turned[e, c] = banks
+            for g in range(passes):
+                for t in range(PACK):
+                    nc.tensor.matmul(
+                        out=turned[e, c][g][:, t, :], lhsT=term[:, g * K_PASS + t : (g + 1) * K_PASS : PACK],
+                        rhs=ident[:], is_transpose=True,
+                        start=(q == 0 and t == 0), stop=(q == PAIRS - 1 and t == PACK - 1),
+                    )
+
+        def copy_slot(e, c):
+            grouped = slot_pool.tile([P, CHUNK_PASSES, B, PACK], BF16, name="grouped", align_bytes=64)
+            for g in range(widths[c] // K_PASS):
+                nc.scalar.copy(out=grouped[:, g, :, :], in_=turned[e, c][g][:].rearrange("p t b -> p b t"))
+            slot_grouped[e, c] = grouped
+
+        def quantise_slot(e, c):
+            passes = widths[c] // K_PASS
+            codes = slot_pool.tile([P, CHUNK_PASSES * B], U32, name="s_codes", align_bytes=64)
+            scales = slot_pool.tile([P, CHUNK_PASSES * B], U8, name="s_scales", align_bytes=64)
+            nc.vector.quantize_mx(
+                out=codes[:, : passes * B].bitcast(FP8X4),
+                scales=scales[:, : passes * B],
+                in_=slot_grouped[e, c][:, :passes, :, :].rearrange("p g b t -> p (g b t)"),
+            )
+            slot_codes[e, c] = codes
+            slot_scales[e, c] = scales
+
+        def multiply(e, k_pass, codes, scales, first_col, opens, closes):
+            piece, w_pass = divmod(e * PASSES + k_pass, W_PASSES)
+            cols = slice(first_col, first_col + B)
+            w_cols = slice(w_pass * H1, (w_pass + 1) * H1)
+            nc.tensor.matmul_mx(
+                out=acc[e][:],
+                lhsT=codes[:, cols].bitcast(FP8X4),
+                lhsT_scale=scales[:, cols],
+                rhs=w_codes[piece][:, w_cols].bitcast(FP8X4),
+                rhs_scale=w_scales[piece][:, w_cols],
+                start=opens,
+                stop=closes,
+            )
+
+        def multiply_unit(e, c):
+            last = c == last_chunk(e)
+            if c == 0:
+                acc[e] = acc_pool.tile([P, H1], F32, name="acc")
             if last:
-                multiply_plain(PASSES - 1, 0)
-                if not half:
-                    multiply_plain(PASSES - 2, PLAIN_HALF_FROM)
+                multiply(e, PASSES - 1, plain_codes[PASSES - 1], plain_scales[PASSES - 1], e * B, False, False)
+                if e >= PLAIN_HALF_FROM:
+                    multiply(
+                        e, PASSES - 2, plain_codes[PASSES - 2], plain_scales[PASSES - 2],
+                        (e - PLAIN_HALF_FROM) * B, False, False,
+                    )
+            passes = widths[c] // K_PASS
             for g in range(passes):
                 multiply(
-                    c * CHUNK_PASSES + g, s_codes, s_scales, slice(g * B, (g + 1) * B),
-                    opens=(c == 0 and g == 0), closes=(last and g == passes - 1),
+                    e, c * CHUNK_PASSES + g, slot_codes[e, c], slot_scales[e, c], g * B,
+                    c == 0 and g == 0, last and g == passes - 1,
                 )
-            if last:
-                layer_norm(e, acc)
-            if u == 3:
-                make_diag()
-            for step in range(next_step, next_step + steps):
-                plain_step(step)
-            next_step += steps
-        mish_and_store(E - 1, E)
+
+        def last_chunk(e):
+            return CHUNKS - 1 if e < PLAIN_HALF_FROM else CHUNKS - 2
+
+        units = [(e, c) for e in range(E) for c in range(last_chunk(e) + 1)]
+
+        side = {}
+
+        def put(i, q, func, *args):
+            side.setdefault((i, q), []).append((func, args))
+
+        for i, (e, c) in enumerate(units):
+            piece = (e * CHUNKS + c) // W_UNITS
+            if c % W_UNITS == 0:
+                if 3 <= piece + 3 < W_PIECES:
+                    put(i, 0, load_w, piece + 3)
+                if piece + 1 < W_PIECES:
+                    put(i, 0, regroup_w, piece + 1)
+                    put(i, 2, quantise_w, piece + 1)
+            if c == last_chunk(e) and e < E - 1:
+                put(i + 3, 0, norm_add, e)
+                put(i + 3, 1, norm_stats, e)
+                put(i + 3, 3, norm_gain, e)
+                put(i + 4, 0, norm_shift, e)
+            if e < 2 and 3 <= c < 7:
+                for k in range(2):
+                    step = 8 * e + 2 * (c - 3) + k
+                    put(i, k, plain_cast, step)
+                    put(i, k + 1, plain_multiply, step)
+                    put(i, 3, plain_copy, step)
+        first_of = {e: units.index((e, 0)) for e in range(E)}
+        put(3, 0, make_diag)
+        put(first_of[0] + 7, 0, plain_quantise, PASSES - 1, 0)
+        put(first_of[1] + 7, 0, plain_quantise, PASSES - 2, PLAIN_HALF_FROM)
+        tail = first_of[E - 1] + 4
+        early = slice(0, (E - 1) * H1)
+        put(tail, 0, mish_exp, early)
+        put(tail + 1, 0, mish_numer, early)
+        put(tail + 1, 1, mish_denom, early)
+        put(tail + 1, 2, mish_times_v, early)
+        put(tail + 2, 0, mish_reciprocal, slice(0, 4 * H1))
+        put(tail + 2, 2, mish_store, 0, 4)
+
+        for step in range(3):
+            load_plain(step)
+        with tc.manual_schedule():
+            for i, (e, c) in enumerate(units):
+                before = units[i - 2] if i >= 2 else None
+                for q in range(PAIRS):
+                    term = scale_even(e, c, q)
+                    if before and q == 0:
+                        copy_slot(*before)
+                    add_odd(term, e, c, q)
+                    if before and q == 1:
+                        quantise_slot(*before)
+                    transpose_term(term, e, c, q)
+                    if before and q == 2:
+                        multiply_unit(*before)
+                    for func, args in side.get((i, q), []):
+                        func(*args)
+            copy_slot(*units[-2])
+            quantise_slot(*units[-2])
+            multiply_unit(*units[-2])
+            copy_slot(*units[-1])
+            mish_reciprocal(slice(4 * H1, (E - 1) * H1))
+            quantise_slot(*units[-1])
+            multiply_unit(*units[-1])
+            mish_store(4, E - 1)
+            last = E - 1
+            cols = slice(last * H1, E * H1)
+            norm_add(last)
+            norm_stats(last)
+            norm_gain(last)
+            norm_shift(last)
+            mish_exp(cols)
+            mish_numer(cols)
+            mish_denom(cols)
+            mish_times_v(cols)
+            mish_reciprocal(cols)
+            mish_store(last, E)

@@ -49,7 +49,8 @@ def tile_softmoedynamics_pa_k_kernel(tc, tokens, logits, W1, b1, g1, be1, out):
         plain_keep = ctx.enter_context(tc.tile_pool(name="plain_keep", bufs=1))
         epi_pool = ctx.enter_context(tc.tile_pool(name="epi", bufs=2))
         mish_pool = ctx.enter_context(tc.tile_pool(name="mish", bufs=1))
-        turned_pool = ctx.enter_context(tc.psum_pool(name="turned", bufs=7))
+        turned_pool = ctx.enter_context(tc.psum_pool(name="turned", bufs=5))
+        plain_psum = ctx.enter_context(tc.psum_pool(name="plain_psum", bufs=2))
         acc_pool = ctx.enter_context(tc.psum_pool(name="acc", bufs=1))
 
         widths = [CHUNK] * (CHUNKS - 1) + [CHUNK - K_PASS]
@@ -96,11 +97,6 @@ def tile_softmoedynamics_pa_k_kernel(tc, tokens, logits, W1, b1, g1, be1, out):
 
         lg = const.tile([P, N, E], BF16)
         nc.sync.dma_start(out=lg[:], in_=logits)
-        for c in range(CHUNKS):
-            for q in range(PAIRS):
-                load_tokens(c, q)
-            if c % W_UNITS == 0 and c // W_UNITS < 3:
-                load_w(c // W_UNITS)
         bias_bc = const.tile([P, E * H1], BF16)
         gain_bc = const.tile([P, E * H1], BF16)
         shift_bc = const.tile([P, E * H1], BF16)
@@ -131,9 +127,6 @@ def tile_softmoedynamics_pa_k_kernel(tc, tokens, logits, W1, b1, g1, be1, out):
         nc.vector.tensor_tensor(
             out=disp[:], in0=disp[:], in1=total[:].unsqueeze(1).to_broadcast([P, N, E]), op=ALU.mult
         )
-
-        regroup_w(0)
-        quantise_w(0)
 
         parked = out.rearrange("b e h -> (b e h)")[0 : B * N * E]
         nc.gpsimd.dma_start(
@@ -180,7 +173,7 @@ def tile_softmoedynamics_pa_k_kernel(tc, tokens, logits, W1, b1, g1, be1, out):
 
         def plain_multiply(step):
             k_pass, first_e, j = plain_steps[step]
-            turned = turned_pool.tile([P, PACK, B], F32, name="turned")
+            turned = plain_psum.tile([P, PACK, B], F32, name="plain_turned")
             for t in range(PACK):
                 nc.tensor.matmul(
                     out=turned[:, t, : (E - first_e) * PLAIN_B],
@@ -369,28 +362,28 @@ def tile_softmoedynamics_pa_k_kernel(tc, tokens, logits, W1, b1, g1, be1, out):
             side.setdefault((i, q), []).append((func, args))
 
         for i, (e, c) in enumerate(units):
-            piece = (e * CHUNKS + c) // W_UNITS
             if c % W_UNITS == 0:
-                if 3 <= piece + 3 < W_PIECES:
-                    put(i, 0, load_w, piece + 3)
-                if piece + 1 < W_PIECES:
-                    put(i, 0, regroup_w, piece + 1)
-                    put(i, 2, quantise_w, piece + 1)
+                piece = (e * CHUNKS + c) // W_UNITS
+                at = min(i + 1, len(units) - 1)
+                put(at, 0, regroup_w, piece)
+                put(at, 2, quantise_w, piece)
+                if 3 <= piece + 2 < W_PIECES:
+                    put(at, 0, load_w, piece + 2)
             if c == last_chunk(e) and e < E - 1:
                 put(i + 3, 0, norm_add, e)
                 put(i + 3, 1, norm_stats, e)
                 put(i + 3, 3, norm_gain, e)
                 put(i + 4, 0, norm_shift, e)
-            if e < 2 and 3 <= c < 7:
+            if e < 2 and 4 <= c < 8:
                 for k in range(2):
-                    step = 8 * e + 2 * (c - 3) + k
+                    step = 8 * e + 2 * (c - 4) + k
                     put(i, k, plain_cast, step)
                     put(i, k + 1, plain_multiply, step)
-                    put(i, 3, plain_copy, step)
+                    put(i + 1, k, plain_copy, step)
         first_of = {e: units.index((e, 0)) for e in range(E)}
         put(3, 0, make_diag)
-        put(first_of[0] + 7, 0, plain_quantise, PASSES - 1, 0)
-        put(first_of[1] + 7, 0, plain_quantise, PASSES - 2, PLAIN_HALF_FROM)
+        put(first_of[1] + 1, 0, plain_quantise, PASSES - 1, 0)
+        put(first_of[2] + 1, 0, plain_quantise, PASSES - 2, PLAIN_HALF_FROM)
         tail = first_of[E - 1] + 4
         early = slice(0, (E - 1) * H1)
         put(tail, 0, mish_exp, early)
@@ -400,15 +393,21 @@ def tile_softmoedynamics_pa_k_kernel(tc, tokens, logits, W1, b1, g1, be1, out):
         put(tail + 2, 0, mish_reciprocal, slice(0, 4 * H1))
         put(tail + 2, 2, mish_store, 0, 4)
 
-        for step in range(3):
-            load_plain(step)
+        for c in range(CHUNKS):
+            for q in range(PAIRS):
+                load_tokens(c, q)
+            if c % W_UNITS == 1 and c // W_UNITS < 3:
+                load_w(c // W_UNITS)
+            if c == 4:
+                for step in range(3):
+                    load_plain(step)
         with tc.manual_schedule():
             for i, (e, c) in enumerate(units):
                 before = units[i - 2] if i >= 2 else None
                 for q in range(PAIRS):
-                    term = scale_even(e, c, q)
                     if before and q == 0:
                         copy_slot(*before)
+                    term = scale_even(e, c, q)
                     add_odd(term, e, c, q)
                     if before and q == 1:
                         quantise_slot(*before)

@@ -25,6 +25,7 @@ W_UNITS = 2
 W_PASSES = W_UNITS * CHUNK_PASSES
 W_PIECES = UNITS // W_UNITS
 PAIRS = N // 2
+RUN = 8
 PLAIN_B = P // N
 PLAIN_J = B // PLAIN_B
 PASSES = D // K_PASS
@@ -42,13 +43,13 @@ def tile_softmoedynamics_pa_k_kernel(tc, tokens, logits, W1, b1, g1, be1, out):
         w_raw_pool = ctx.enter_context(tc.tile_pool(name="w_raw", bufs=3))
         w_grp_pool = ctx.enter_context(tc.tile_pool(name="w_grp", bufs=2))
         w_mx_pool = ctx.enter_context(tc.tile_pool(name="w_mx", bufs=3))
+        product_pool = ctx.enter_context(tc.tile_pool(name="product", bufs=3))
         term_pool = ctx.enter_context(tc.tile_pool(name="term", bufs=7))
         slot_pool = ctx.enter_context(tc.tile_pool(name="slot", bufs=3))
         plain_pool = ctx.enter_context(tc.tile_pool(name="plain", bufs=2))
         plain_raw_pool = ctx.enter_context(tc.tile_pool(name="plain_raw", bufs=4))
         plain_keep = ctx.enter_context(tc.tile_pool(name="plain_keep", bufs=1))
         epi_pool = ctx.enter_context(tc.tile_pool(name="epi", bufs=2))
-        mish_pool = ctx.enter_context(tc.tile_pool(name="mish", bufs=1))
         turned_pool = ctx.enter_context(tc.psum_pool(name="turned", bufs=5))
         plain_psum = ctx.enter_context(tc.psum_pool(name="plain_psum", bufs=2))
         acc_pool = ctx.enter_context(tc.psum_pool(name="acc", bufs=1))
@@ -168,8 +169,8 @@ def tile_softmoedynamics_pa_k_kernel(tc, tokens, logits, W1, b1, g1, be1, out):
             words = plain_pool.tile([P, PACK, P], F32, name="words")
             nc.vector.tensor_copy(out=words[:], in_=plain_raw[step][:].rearrange("p (w t) -> p t w", t=PACK))
             plain_words[step] = words
-            if step + 3 < len(plain_steps):
-                load_plain(step + 3)
+            if step + 4 < len(plain_steps):
+                load_plain(step + 4)
 
         def plain_multiply(step):
             k_pass, first_e, j = plain_steps[step]
@@ -241,28 +242,38 @@ def tile_softmoedynamics_pa_k_kernel(tc, tokens, logits, W1, b1, g1, be1, out):
                 op0=ALU.mult, op1=ALU.add,
             )
 
-        w_exp = mish_pool.tile([P, E * H1], F32)
-        numer = mish_pool.tile([P, E * H1], F32)
+        mish_scratch = {}
+
+        def mish_begin():
+            scratch = plain_keep.tile([P, 2, E * H1], F32, name="plain_grouped", align_bytes=64)
+            mish_scratch["w"] = scratch[:, 0, :]
+            mish_scratch["numer"] = scratch[:, 1, :]
 
         def mish_exp(cols):
+            w_exp, numer = mish_scratch["w"], mish_scratch["numer"]
             nc.vector.tensor_scalar_min(out=w_exp[:, cols], in0=v[:, cols], scalar1=MISH_CLAMP)
             nc.scalar.activation(out=w_exp[:, cols], in_=w_exp[:, cols], func=ACT.Exp)
 
         def mish_numer(cols):
+            w_exp, numer = mish_scratch["w"], mish_scratch["numer"]
             nc.vector.scalar_tensor_tensor(
                 out=numer[:, cols], in0=w_exp[:, cols], scalar=2.0, in1=w_exp[:, cols], op0=ALU.add, op1=ALU.mult
             )
 
         def mish_denom(cols):
+            w_exp, numer = mish_scratch["w"], mish_scratch["numer"]
             nc.vector.tensor_scalar_add(out=w_exp[:, cols], in0=numer[:, cols], scalar1=2.0)
 
         def mish_times_v(cols):
+            w_exp, numer = mish_scratch["w"], mish_scratch["numer"]
             nc.vector.tensor_tensor(out=numer[:, cols], in0=numer[:, cols], in1=v[:, cols], op=ALU.mult)
 
         def mish_reciprocal(cols):
+            w_exp, numer = mish_scratch["w"], mish_scratch["numer"]
             nc.vector.reciprocal(out=w_exp[:, cols], in_=w_exp[:, cols])
 
         def mish_store(first_e, last_e):
+            w_exp, numer = mish_scratch["w"], mish_scratch["numer"]
             cols = slice(first_e * H1, last_e * H1)
             nc.vector.tensor_tensor(out=numer[:, cols], in0=numer[:, cols], in1=w_exp[:, cols], op=ALU.mult)
             nc.sync.dma_start(
@@ -274,31 +285,52 @@ def tile_softmoedynamics_pa_k_kernel(tc, tokens, logits, W1, b1, g1, be1, out):
         slot_codes = {}
         slot_scales = {}
 
-        def scale_even(e, c, q):
-            term = term_pool.tile([P, CHUNK], F32, name="term")
+        def tokens_by_code(c, n):
+            return tok[c][:, n, :].rearrange("p (w t) -> p t w", t=PACK)
+
+        def new_term(c):
+            term = term_pool.tile([P, PACK, CHUNK // PACK], F32, name="term")
+            return term[:, :, : widths[c] // PACK]
+
+        def vector_product(e, c, n):
+            term = new_term(c)
+            nc.vector.tensor_scalar_mul(out=term, in0=tokens_by_code(c, n), scalar1=disp[:, n, e : e + 1])
+            return term
+
+        def scalar_product(e, c, n):
+            term = new_term(c)
             nc.scalar.activation(
-                out=term[:, : widths[c]], in_=tok[c][:, 2 * q, :], func=ACT.Copy, scale=disp[:, 2 * q, e : e + 1]
+                out=term.rearrange("p t (w i) -> p w t i", i=RUN),
+                in_=tok[c][:, n, :].rearrange("p (w i t) -> p w t i", i=RUN, t=PACK),
+                func=ACT.Copy, scale=disp[:, n, e : e + 1],
             )
             return term
 
-        def add_odd(term, e, c, q):
-            made = term[:, : widths[c]]
+        def scalar_half(e, c, n):
+            product = product_pool.tile([P, CHUNK], F32, name="product")
+            nc.scalar.activation(
+                out=product[:, : widths[c]], in_=tok[c][:, n, :], func=ACT.Copy, scale=disp[:, n, e : e + 1]
+            )
+            return product
+
+        def vector_half(product, e, c, n):
+            term = new_term(c)
             nc.vector.scalar_tensor_tensor(
-                out=made, in0=tok[c][:, 2 * q + 1, :], scalar=disp[:, 2 * q + 1, e : e + 1], in1=made,
+                out=term.rearrange("p t w -> p w t"),
+                in0=tok[c][:, n, :].rearrange("p (w t) -> p w t", t=PACK),
+                scalar=disp[:, n, e : e + 1],
+                in1=product[:, : widths[c]].rearrange("p (w t) -> p w t", t=PACK),
                 op0=ALU.mult, op1=ALU.add,
             )
+            return term
 
-        def transpose_term(term, e, c, q):
-            passes = widths[c] // K_PASS
-            if q == 0:
-                banks = [turned_pool.tile([P, PACK, B], F32, name="turned") for g in range(passes)]
-                turned[e, c] = banks
-            for g in range(passes):
+        def transpose_term(term, e, c, opens, closes):
+            for g in range(widths[c] // K_PASS):
                 for t in range(PACK):
                     nc.tensor.matmul(
-                        out=turned[e, c][g][:, t, :], lhsT=term[:, g * K_PASS + t : (g + 1) * K_PASS : PACK],
+                        out=turned[e, c][g][:, t, :], lhsT=term[:, t, g * P : (g + 1) * P],
                         rhs=ident[:], is_transpose=True,
-                        start=(q == 0 and t == 0), stop=(q == PAIRS - 1 and t == PACK - 1),
+                        start=(opens and t == 0), stop=(closes and t == PACK - 1),
                     )
 
         def copy_slot(e, c):
@@ -351,6 +383,19 @@ def tile_softmoedynamics_pa_k_kernel(tc, tokens, logits, W1, b1, g1, be1, out):
                     c == 0 and g == 0, last and g == passes - 1,
                 )
 
+        def keep_warm(e, c, banks):
+            piece = (e * CHUNKS + c) // W_UNITS
+            for bank in banks:
+                nc.tensor.matmul_mx(
+                    out=bank[:].rearrange("p t b -> p (t b)"),
+                    lhsT=slot_codes[e, c][:, :B].bitcast(FP8X4),
+                    lhsT_scale=slot_scales[e, c][:, :B],
+                    rhs=w_codes[piece][:].bitcast(FP8X4),
+                    rhs_scale=w_scales[piece][:],
+                    start=True,
+                    stop=True,
+                )
+
         def last_chunk(e):
             return CHUNKS - 1 if e < PLAIN_HALF_FROM else CHUNKS - 2
 
@@ -386,6 +431,7 @@ def tile_softmoedynamics_pa_k_kernel(tc, tokens, logits, W1, b1, g1, be1, out):
         put(first_of[2] + 1, 0, plain_quantise, PASSES - 2, PLAIN_HALF_FROM)
         tail = first_of[E - 1] + 4
         early = slice(0, (E - 1) * H1)
+        put(tail, 0, mish_begin)
         put(tail, 0, mish_exp, early)
         put(tail + 1, 0, mish_numer, early)
         put(tail + 1, 1, mish_denom, early)
@@ -399,19 +445,30 @@ def tile_softmoedynamics_pa_k_kernel(tc, tokens, logits, W1, b1, g1, be1, out):
             if c % W_UNITS == 1 and c // W_UNITS < 3:
                 load_w(c // W_UNITS)
             if c == 4:
-                for step in range(3):
+                for step in range(4):
                     load_plain(step)
         with tc.manual_schedule():
             for i, (e, c) in enumerate(units):
                 before = units[i - 2] if i >= 2 else None
                 for q in range(PAIRS):
+                    even, odd = 2 * q, 2 * q + 1
                     if before and q == 0:
                         copy_slot(*before)
-                    term = scale_even(e, c, q)
-                    add_odd(term, e, c, q)
+                    if q == 0:
+                        terms = [vector_product(e, c, even), vector_product(e, c, odd)]
+                    elif q == 2:
+                        terms = [scalar_product(e, c, even), vector_product(e, c, odd)]
+                    else:
+                        terms = [vector_half(scalar_half(e, c, even), e, c, odd)]
                     if before and q == 1:
                         quantise_slot(*before)
-                    transpose_term(term, e, c, q)
+                    if q == 0:
+                        banks = [turned_pool.tile([P, PACK, B], F32, name="turned") for g in range(widths[c] // K_PASS)]
+                        turned[e, c] = banks
+                        if i >= 3:
+                            keep_warm(*units[i - 3], banks)
+                    for k, term in enumerate(terms):
+                        transpose_term(term, e, c, q == 0 and k == 0, q == PAIRS - 1)
                     if before and q == 2:
                         multiply_unit(*before)
                     for func, args in side.get((i, q), []):

@@ -45,7 +45,7 @@ def tile_softmoedynamics_pa_k_kernel(tc, tokens, logits, W1, b1, g1, be1, out):
         w_mx_pool = ctx.enter_context(tc.tile_pool(name="w_mx", bufs=3))
         product_pool = ctx.enter_context(tc.tile_pool(name="product", bufs=3))
         term_pool = ctx.enter_context(tc.tile_pool(name="term", bufs=7))
-        slot_pool = ctx.enter_context(tc.tile_pool(name="slot", bufs=3))
+        slot_pool = ctx.enter_context(tc.tile_pool(name="slot", bufs=2))
         plain_pool = ctx.enter_context(tc.tile_pool(name="plain", bufs=2))
         plain_raw_pool = ctx.enter_context(tc.tile_pool(name="plain_raw", bufs=4))
         plain_keep = ctx.enter_context(tc.tile_pool(name="plain_keep", bufs=1))
@@ -341,8 +341,8 @@ def tile_softmoedynamics_pa_k_kernel(tc, tokens, logits, W1, b1, g1, be1, out):
 
         def quantise_slot(e, c):
             passes = widths[c] // K_PASS
-            codes = slot_pool.tile([P, CHUNK_PASSES * B], U32, name="s_codes", align_bytes=64)
-            scales = slot_pool.tile([P, CHUNK_PASSES * B], U8, name="s_scales", align_bytes=64)
+            codes = slot_pool.tile([P, CHUNK_PASSES * B], U32, name="s_codes", align_bytes=64, bufs=4)
+            scales = slot_pool.tile([P, CHUNK_PASSES * B], U8, name="s_scales", align_bytes=64, bufs=4)
             nc.vector.quantize_mx(
                 out=codes[:, : passes * B].bitcast(FP8X4),
                 scales=scales[:, : passes * B],
@@ -409,16 +409,16 @@ def tile_softmoedynamics_pa_k_kernel(tc, tokens, logits, W1, b1, g1, be1, out):
         for i, (e, c) in enumerate(units):
             if c % W_UNITS == 0:
                 piece = (e * CHUNKS + c) // W_UNITS
-                at = min(i + 1, len(units) - 1)
+                at = min(i + 2, len(units) - 1)
                 put(at, 0, regroup_w, piece)
                 put(at, 2, quantise_w, piece)
                 if 3 <= piece + 2 < W_PIECES:
                     put(at, 0, load_w, piece + 2)
             if c == last_chunk(e) and e < E - 1:
-                put(i + 3, 0, norm_add, e)
-                put(i + 3, 1, norm_stats, e)
-                put(i + 3, 3, norm_gain, e)
-                put(i + 4, 0, norm_shift, e)
+                put(i + 3, 1, norm_add, e)
+                put(i + 3, 2, norm_stats, e)
+                put(i + 4, 0, norm_gain, e)
+                put(i + 4, 1, norm_shift, e)
             if e < 2 and 4 <= c < 8:
                 for k in range(2):
                     step = 8 * e + 2 * (c - 4) + k
@@ -454,10 +454,10 @@ def tile_softmoedynamics_pa_k_kernel(tc, tokens, logits, W1, b1, g1, be1, out):
                     even, odd = 2 * q, 2 * q + 1
                     if before and q == 0:
                         copy_slot(*before)
-                    if q == 0:
-                        terms = [vector_product(e, c, even), vector_product(e, c, odd)]
-                    elif q == 2:
+                    if q == 2 or (q == 0 and c % 2 == 1):
                         terms = [scalar_product(e, c, even), vector_product(e, c, odd)]
+                    elif q == 0:
+                        terms = [vector_product(e, c, even), vector_product(e, c, odd)]
                     else:
                         terms = [vector_half(scalar_half(e, c, even), e, c, odd)]
                     if before and q == 1:
@@ -466,13 +466,13 @@ def tile_softmoedynamics_pa_k_kernel(tc, tokens, logits, W1, b1, g1, be1, out):
                         banks = [turned_pool.tile([P, PACK, B], F32, name="turned") for g in range(widths[c] // K_PASS)]
                         turned[e, c] = banks
                         if i >= 3:
+                            multiply_unit(*units[i - 3])
                             keep_warm(*units[i - 3], banks)
                     for k, term in enumerate(terms):
                         transpose_term(term, e, c, q == 0 and k == 0, q == PAIRS - 1)
-                    if before and q == 2:
-                        multiply_unit(*before)
                     for func, args in side.get((i, q), []):
                         func(*args)
+            multiply_unit(*units[-3])
             copy_slot(*units[-2])
             quantise_slot(*units[-2])
             multiply_unit(*units[-2])

@@ -42,15 +42,16 @@ def tile_softmoedynamics_pa_k_kernel(tc, tokens, logits, W1, b1, g1, be1, out):
         tok_pool = ctx.enter_context(tc.tile_pool(name="tok", bufs=1))
         w_raw_pool = ctx.enter_context(tc.tile_pool(name="w_raw", bufs=3))
         w_grp_pool = ctx.enter_context(tc.tile_pool(name="w_grp", bufs=2))
-        w_mx_pool = ctx.enter_context(tc.tile_pool(name="w_mx", bufs=3))
+        w_mx_pool = ctx.enter_context(tc.tile_pool(name="w_mx", bufs=2))
         product_pool = ctx.enter_context(tc.tile_pool(name="product", bufs=3))
         term_pool = ctx.enter_context(tc.tile_pool(name="term", bufs=7))
         slot_pool = ctx.enter_context(tc.tile_pool(name="slot", bufs=2))
         plain_pool = ctx.enter_context(tc.tile_pool(name="plain", bufs=2))
-        plain_raw_pool = ctx.enter_context(tc.tile_pool(name="plain_raw", bufs=4))
+        plain_raw_pool = ctx.enter_context(tc.tile_pool(name="plain_raw", bufs=6))
         plain_keep = ctx.enter_context(tc.tile_pool(name="plain_keep", bufs=1))
         epi_pool = ctx.enter_context(tc.tile_pool(name="epi", bufs=2))
-        turned_pool = ctx.enter_context(tc.psum_pool(name="turned", bufs=5))
+        turned_pool = ctx.enter_context(tc.psum_pool(name="turned", bufs=4))
+        unread_pool = ctx.enter_context(tc.psum_pool(name="unread", bufs=1))
         plain_psum = ctx.enter_context(tc.psum_pool(name="plain_psum", bufs=2))
         acc_pool = ctx.enter_context(tc.psum_pool(name="acc", bufs=1))
 
@@ -169,8 +170,8 @@ def tile_softmoedynamics_pa_k_kernel(tc, tokens, logits, W1, b1, g1, be1, out):
             words = plain_pool.tile([P, PACK, P], F32, name="words")
             nc.vector.tensor_copy(out=words[:], in_=plain_raw[step][:].rearrange("p (w t) -> p t w", t=PACK))
             plain_words[step] = words
-            if step + 4 < len(plain_steps):
-                load_plain(step + 4)
+            if step + 6 < len(plain_steps):
+                load_plain(step + 6)
 
         def plain_multiply(step):
             k_pass, first_e, j = plain_steps[step]
@@ -333,10 +334,10 @@ def tile_softmoedynamics_pa_k_kernel(tc, tokens, logits, W1, b1, g1, be1, out):
                         start=(opens and t == 0), stop=(closes and t == PACK - 1),
                     )
 
-        def copy_slot(e, c):
+        def copy_slot(e, c, copies=(nc.scalar.copy, nc.scalar.copy)):
             grouped = slot_pool.tile([P, CHUNK_PASSES, B, PACK], BF16, name="grouped", align_bytes=64)
             for g in range(widths[c] // K_PASS):
-                nc.scalar.copy(out=grouped[:, g, :, :], in_=turned[e, c][g][:].rearrange("p t b -> p b t"))
+                copies[g](out=grouped[:, g, :, :], in_=turned[e, c][g][:].rearrange("p t b -> p b t"))
             slot_grouped[e, c] = grouped
 
         def quantise_slot(e, c):
@@ -383,18 +384,19 @@ def tile_softmoedynamics_pa_k_kernel(tc, tokens, logits, W1, b1, g1, be1, out):
                     c == 0 and g == 0, last and g == passes - 1,
                 )
 
-        def keep_warm(e, c, banks):
+        unread = unread_pool.tile([P, W_PASSES * H1], F32)
+
+        def keep_warm(e, c):
             piece = (e * CHUNKS + c) // W_UNITS
-            for bank in banks:
-                nc.tensor.matmul_mx(
-                    out=bank[:].rearrange("p t b -> p (t b)"),
-                    lhsT=slot_codes[e, c][:, :B].bitcast(FP8X4),
-                    lhsT_scale=slot_scales[e, c][:, :B],
-                    rhs=w_codes[piece][:].bitcast(FP8X4),
-                    rhs_scale=w_scales[piece][:],
-                    start=True,
-                    stop=True,
-                )
+            nc.tensor.matmul_mx(
+                out=unread[:],
+                lhsT=slot_codes[e, c][:, :B].bitcast(FP8X4),
+                lhsT_scale=slot_scales[e, c][:, :B],
+                rhs=w_codes[piece][:].bitcast(FP8X4),
+                rhs_scale=w_scales[piece][:],
+                start=True,
+                stop=True,
+            )
 
         def last_chunk(e):
             return CHUNKS - 1 if e < PLAIN_HALF_FROM else CHUNKS - 2
@@ -409,7 +411,7 @@ def tile_softmoedynamics_pa_k_kernel(tc, tokens, logits, W1, b1, g1, be1, out):
         for i, (e, c) in enumerate(units):
             if c % W_UNITS == 0:
                 piece = (e * CHUNKS + c) // W_UNITS
-                at = min(i + 2, len(units) - 1)
+                at = min(i + 2, len(units) - (1 if c == last_chunk(e) else 2))
                 put(at, 0, regroup_w, piece)
                 put(at, 2, quantise_w, piece)
                 if 3 <= piece + 2 < W_PIECES:
@@ -444,12 +446,13 @@ def tile_softmoedynamics_pa_k_kernel(tc, tokens, logits, W1, b1, g1, be1, out):
                 load_tokens(c, q)
             if c % W_UNITS == 1 and c // W_UNITS < 3:
                 load_w(c // W_UNITS)
-            if c == 4:
-                for step in range(4):
+            if c in (4, 6):
+                for step in range(4) if c == 4 else range(4, 6):
                     load_plain(step)
         with tc.manual_schedule():
             for i, (e, c) in enumerate(units):
                 before = units[i - 2] if i >= 2 else None
+                done = 0
                 for q in range(PAIRS):
                     even, odd = 2 * q, 2 * q + 1
                     if before and q == 0:
@@ -467,25 +470,28 @@ def tile_softmoedynamics_pa_k_kernel(tc, tokens, logits, W1, b1, g1, be1, out):
                         turned[e, c] = banks
                         if i >= 3:
                             multiply_unit(*units[i - 3])
-                            keep_warm(*units[i - 3], banks)
-                    for k, term in enumerate(terms):
-                        transpose_term(term, e, c, q == 0 and k == 0, q == PAIRS - 1)
+                    for term in terms:
+                        if i >= 3 and done % 2 == 0:
+                            keep_warm(*units[i - 3])
+                        transpose_term(term, e, c, done == 0, q == PAIRS - 1)
+                        done += 1
                     for func, args in side.get((i, q), []):
                         func(*args)
             multiply_unit(*units[-3])
             copy_slot(*units[-2])
             quantise_slot(*units[-2])
             multiply_unit(*units[-2])
-            copy_slot(*units[-1])
-            mish_reciprocal(slice(4 * H1, (E - 1) * H1))
+            mish_reciprocal(slice(4 * H1, 6 * H1))
+            copy_slot(*units[-1], copies=(nc.scalar.copy, nc.vector.tensor_copy))
             quantise_slot(*units[-1])
             multiply_unit(*units[-1])
-            mish_store(4, E - 1)
             last = E - 1
             cols = slice(last * H1, E * H1)
+            mish_reciprocal(slice(6 * H1, last * H1))
             norm_add(last)
             norm_stats(last)
             norm_gain(last)
+            mish_store(4, last)
             norm_shift(last)
             mish_exp(cols)
             mish_numer(cols)

@@ -43,8 +43,7 @@ def tile_softmoedynamics_pa_k_kernel(tc, tokens, logits, W1, b1, g1, be1, out):
         w_raw_pool = ctx.enter_context(tc.tile_pool(name="w_raw", bufs=3))
         w_grp_pool = ctx.enter_context(tc.tile_pool(name="w_grp", bufs=2))
         w_mx_pool = ctx.enter_context(tc.tile_pool(name="w_mx", bufs=2))
-        product_pool = ctx.enter_context(tc.tile_pool(name="product", bufs=3))
-        term_pool = ctx.enter_context(tc.tile_pool(name="term", bufs=7))
+        term_pool = ctx.enter_context(tc.tile_pool(name="term", bufs=9))
         slot_pool = ctx.enter_context(tc.tile_pool(name="slot", bufs=2))
         plain_pool = ctx.enter_context(tc.tile_pool(name="plain", bufs=2))
         plain_raw_pool = ctx.enter_context(tc.tile_pool(name="plain_raw", bufs=6))
@@ -307,20 +306,9 @@ def tile_softmoedynamics_pa_k_kernel(tc, tokens, logits, W1, b1, g1, be1, out):
             )
             return term
 
-        def scalar_half(e, c, n):
-            product = product_pool.tile([P, CHUNK], F32, name="product")
-            nc.scalar.activation(
-                out=product[:, : widths[c]], in_=tok[c][:, n, :], func=ACT.Copy, scale=disp[:, n, e : e + 1]
-            )
-            return product
-
-        def vector_half(product, e, c, n):
-            term = new_term(c)
+        def vector_add(term, e, c, n):
             nc.vector.scalar_tensor_tensor(
-                out=term.rearrange("p t w -> p w t"),
-                in0=tok[c][:, n, :].rearrange("p (w t) -> p w t", t=PACK),
-                scalar=disp[:, n, e : e + 1],
-                in1=product[:, : widths[c]].rearrange("p (w t) -> p w t", t=PACK),
+                out=term, in0=tokens_by_code(c, n), scalar=disp[:, n, e : e + 1], in1=term,
                 op0=ALU.mult, op1=ALU.add,
             )
             return term
@@ -421,12 +409,15 @@ def tile_softmoedynamics_pa_k_kernel(tc, tokens, logits, W1, b1, g1, be1, out):
                 put(i + 3, 2, norm_stats, e)
                 put(i + 4, 0, norm_gain, e)
                 put(i + 4, 1, norm_shift, e)
-            if e < 2 and 4 <= c < 8:
-                for k in range(2):
-                    step = 8 * e + 2 * (c - 4) + k
-                    put(i, k, plain_cast, step)
-                    put(i, k + 1, plain_multiply, step)
-                    put(i + 1, k, plain_copy, step)
+            steps = []
+            if e == 0 and c >= 4:
+                steps = [2 * (c - 4), 2 * (c - 4) + 1]
+            elif e == 1 and c >= 1:
+                steps = [PLAIN_J, PLAIN_J + 1] if c == 1 else [PLAIN_J + c]
+            for k, step in enumerate(steps):
+                put(i, k, plain_cast, step)
+                put(i, k + 1, plain_multiply, step)
+                put(i + 1, k, plain_copy, step)
         first_of = {e: units.index((e, 0)) for e in range(E)}
         put(3, 0, make_diag)
         put(first_of[1] + 1, 0, plain_quantise, PASSES - 1, 0)
@@ -462,7 +453,7 @@ def tile_softmoedynamics_pa_k_kernel(tc, tokens, logits, W1, b1, g1, be1, out):
                     elif q == 0:
                         terms = [vector_product(e, c, even), vector_product(e, c, odd)]
                     else:
-                        terms = [vector_half(scalar_half(e, c, even), e, c, odd)]
+                        terms = [vector_add(scalar_product(e, c, even), e, c, odd)]
                     if before and q == 1:
                         quantise_slot(*before)
                     if q == 0:
@@ -470,9 +461,9 @@ def tile_softmoedynamics_pa_k_kernel(tc, tokens, logits, W1, b1, g1, be1, out):
                         turned[e, c] = banks
                         if i >= 3:
                             multiply_unit(*units[i - 3])
-                    for term in terms:
-                        if i >= 3 and done % 2 == 0:
                             keep_warm(*units[i - 3])
+                            keep_warm(*units[i - 3])
+                    for term in terms:
                         transpose_term(term, e, c, done == 0, q == PAIRS - 1)
                         done += 1
                     for func, args in side.get((i, q), []):

from contextlib import ExitStack

import concourse.mybir as mybir
from concourse.masks import make_identity

F32 = mybir.dt.float32
BF16 = mybir.dt.bfloat16
U32 = mybir.dt.uint32
U8 = mybir.dt.uint8
FP8X4 = mybir.dt.float8_e4m3fn_x4
ALU = mybir.AluOpType
ACT = mybir.ActivationFunctionType
AXIS = mybir.AxisListType

B, N, E, D, H1 = 128, 8, 8, 8192, 128
EPS = 1e-5
P = 128
PACK = 4
K_PASS = P * PACK
CHUNK = 1024
CHUNKS = D // CHUNK
CHUNK_PASSES = CHUNK // K_PASS
UNITS = E * CHUNKS
W_UNITS = 2
W_PASSES = W_UNITS * CHUNK_PASSES
W_PIECES = UNITS // W_UNITS
PAIRS = N // 2
RUN = 8
PLAIN_B = P // N
PLAIN_J = B // PLAIN_B
PASSES = D // K_PASS
PLAIN_HALF_FROM = E // 2
MISH_CLAMP = 20.0

FLOPS = 2 * E * B * D * H1 + 2 * B * N * E * D


def tile_softmoedynamics_pa_k_kernel(tc, tokens, logits, W1, b1, g1, be1, out):
    nc = tc.nc
    with ExitStack() as ctx:
        const = ctx.enter_context(tc.tile_pool(name="const", bufs=1))
        tok_pool = ctx.enter_context(tc.tile_pool(name="tok", bufs=1))
        w_raw_pool = ctx.enter_context(tc.tile_pool(name="w_raw", bufs=3))
        w_grp_pool = ctx.enter_context(tc.tile_pool(name="w_grp", bufs=2))
        w_mx_pool = ctx.enter_context(tc.tile_pool(name="w_mx", bufs=2))
        term_pool = ctx.enter_context(tc.tile_pool(name="term", bufs=9))
        slot_pool = ctx.enter_context(tc.tile_pool(name="slot", bufs=2))
        plain_pool = ctx.enter_context(tc.tile_pool(name="plain", bufs=2))
        plain_raw_pool = ctx.enter_context(tc.tile_pool(name="plain_raw", bufs=6))
        plain_keep = ctx.enter_context(tc.tile_pool(name="plain_keep", bufs=1))
        epi_pool = ctx.enter_context(tc.tile_pool(name="epi", bufs=2))
        turned_pool = ctx.enter_context(tc.psum_pool(name="turned", bufs=4))
        unread_pool = ctx.enter_context(tc.psum_pool(name="unread", bufs=1))
        plain_psum = ctx.enter_context(tc.psum_pool(name="plain_psum", bufs=2))
        acc_pool = ctx.enter_context(tc.psum_pool(name="acc", bufs=1))

        widths = [CHUNK] * (CHUNKS - 1) + [CHUNK - K_PASS]
        tok = [tok_pool.tile([P, N, widths[c]], BF16, name="tok%d" % c) for c in range(CHUNKS)]

        def load_tokens(c, q):
            agents = slice(2 * q, 2 * q + 2)
            nc.sync.dma_start(
                out=tok[c][:, agents, :], in_=tokens[:, agents, c * CHUNK : c * CHUNK + widths[c]]
            )

        w_raw = {}
        w_grouped = {}
        w_codes = {}
        w_scales = {}

        def load_w(piece):
            first = piece * W_PASSES * K_PASS
            raw = w_raw_pool.tile([P, PACK, W_PASSES * H1], BF16, name="w_raw")
            rows = W1.rearrange("e d h -> (e d) h")[first : first + W_PASSES * K_PASS, :]
            by_code = rows.rearrange("(g p t) h -> t p g h", t=PACK, p=P)
            for t in range(PACK):
                nc.sync.dma_start(
                    out=raw[:, t, :].rearrange("p (g h) -> p g h", h=H1), in_=by_code[t]
                )
            w_raw[piece] = raw

        def regroup_w(piece):
            grouped = w_grp_pool.tile([P, W_PASSES * H1, PACK], BF16, name="w_grp", align_bytes=64)
            nc.vector.tensor_copy(
                out=grouped[:].rearrange("p (c i) t -> p c t i", i=4),
                in_=w_raw[piece][:].rearrange("p t (c i) -> p c t i", i=4),
            )
            w_grouped[piece] = grouped

        def quantise_w(piece):
            w_codes[piece] = w_mx_pool.tile([P, W_PASSES * H1], U32, name="w_codes", align_bytes=64)
            w_scales[piece] = w_mx_pool.tile([P, W_PASSES * H1], U8, name="w_scales", align_bytes=64)
            nc.vector.quantize_mx(
                out=w_codes[piece][:].bitcast(FP8X4),
                scales=w_scales[piece][:],
                in_=w_grouped[piece][:].rearrange("p w t -> p (w t)"),
            )

        lg = const.tile([P, N, E], BF16)
        nc.sync.dma_start(out=lg[:], in_=logits)
        bias_bc = const.tile([P, E * H1], BF16)
        gain_bc = const.tile([P, E * H1], BF16)
        shift_bc = const.tile([P, E * H1], BF16)
        for row_bc, vec in ((bias_bc, b1), (gain_bc, g1), (shift_bc, be1)):
            nc.gpsimd.dma_start(
                out=row_bc[:], in_=vec.rearrange("e h -> (e h)").partition_broadcast(P)
            )

        ident = const.tile([P, P], F32)
        make_identity(nc, ident[:])
        minus_half = const.tile([P, 1], F32)
        nc.vector.memset(minus_half[:], -0.5)
        warm = const.tile([P, 1], F32)
        nc.scalar.activation(out=warm[:], in_=minus_half[:], func=ACT.Exp)

        top = const.tile([P, E], F32)
        nc.vector.tensor_reduce(out=top[:], in_=lg[:].rearrange("p n e -> p e n"), axis=AXIS.X, op=ALU.max)
        disp = const.tile([P, N, E], F32)
        nc.vector.tensor_tensor(
            out=disp[:], in0=lg[:], in1=top[:].unsqueeze(1).to_broadcast([P, N, E]), op=ALU.subtract
        )
        nc.scalar.activation(out=disp[:], in_=disp[:], func=ACT.Exp)
        total = const.tile([P, E], F32)
        nc.vector.tensor_reduce(
            out=total[:], in_=disp[:].rearrange("p n e -> p e n"), axis=AXIS.X, op=ALU.add
        )
        nc.vector.reciprocal(out=total[:], in_=total[:])
        nc.vector.tensor_tensor(
            out=disp[:], in0=disp[:], in1=total[:].unsqueeze(1).to_broadcast([P, N, E]), op=ALU.mult
        )

        parked = out.rearrange("b e h -> (b e h)")[0 : B * N * E]
        nc.gpsimd.dma_start(
            out=parked.rearrange("(b x) -> b x", x=N * E), in_=disp[:].rearrange("p n e -> p (n e)")
        )
        disp_rows = const.tile([P, PLAIN_J, E], F32)
        nc.gpsimd.dma_start(out=disp_rows[:], in_=parked.rearrange("(j p e) -> p j e", p=P, e=E))
        own = const.tile([P, PLAIN_B], F32)
        nc.vector.tensor_reduce(
            out=own[:], in_=ident[:].rearrange("p (b n) -> p b n", n=N), axis=AXIS.X, op=ALU.add
        )
        diag = const.tile([P, PLAIN_J * E, PLAIN_B], F32)

        def make_diag():
            nc.gpsimd.tensor_tensor(
                out=diag[:],
                in0=disp_rows[:].rearrange("p j e -> p (j e)").unsqueeze(2).to_broadcast([P, PLAIN_J * E, PLAIN_B]),
                in1=own[:].unsqueeze(1).to_broadcast([P, PLAIN_J * E, PLAIN_B]),
                op=ALU.mult,
            )

        plain_steps = [(PASSES - 1, 0, j) for j in range(PLAIN_J)]
        plain_steps += [(PASSES - 2, PLAIN_HALF_FROM, j) for j in range(PLAIN_J)]
        plain_raw = {}
        plain_words = {}
        plain_turned = {}
        plain_grouped = {}
        plain_codes = {}
        plain_scales = {}

        def load_plain(step):
            k_pass, first_e, j = plain_steps[step]
            raw = plain_raw_pool.tile([P, K_PASS], BF16, name="plain_raw")
            rows = tokens.rearrange("(j b) n d -> j (b n) d", b=PLAIN_B)[j]
            nc.sync.dma_start(out=raw[:], in_=rows[:, k_pass * K_PASS : (k_pass + 1) * K_PASS])
            plain_raw[step] = raw

        def plain_cast(step):
            words = plain_pool.tile([P, PACK, P], F32, name="words")
            nc.vector.tensor_copy(out=words[:], in_=plain_raw[step][:].rearrange("p (w t) -> p t w", t=PACK))
            plain_words[step] = words
            if step + 6 < len(plain_steps):
                load_plain(step + 6)

        def plain_multiply(step):
            k_pass, first_e, j = plain_steps[step]
            turned = plain_psum.tile([P, PACK, B], F32, name="plain_turned")
            for t in range(PACK):
                nc.tensor.matmul(
                    out=turned[:, t, : (E - first_e) * PLAIN_B],
                    lhsT=plain_words[step][:, t, :],
                    rhs=diag[:, j * E + first_e : (j + 1) * E, :].rearrange("p e b -> p (e b)"),
                    start=True,
                    stop=True,
                )
            plain_turned[step] = turned

        def plain_copy(step):
            k_pass, first_e, j = plain_steps[step]
            experts = E - first_e
            if j == 0:
                plain_grouped[k_pass] = plain_keep.tile([P, experts, B, PACK], BF16, name="plain_grouped", align_bytes=64)
            nc.scalar.copy(
                out=plain_grouped[k_pass][:, :, j * PLAIN_B : (j + 1) * PLAIN_B, :],
                in_=plain_turned[step][:, :, : experts * PLAIN_B].rearrange("p t (e b) -> p e b t", b=PLAIN_B),
            )

        def plain_quantise(k_pass, first_e):
            experts = E - first_e
            codes = plain_keep.tile([P, experts * B], U32, name="plain_codes%d" % k_pass, align_bytes=64)
            scales = plain_keep.tile([P, experts * B], U8, name="plain_scales%d" % k_pass, align_bytes=64)
            nc.vector.quantize_mx(
                out=codes[:].bitcast(FP8X4),
                scales=scales[:],
                in_=plain_grouped[k_pass][:].rearrange("p e b t -> p (e b t)"),
            )
            plain_codes[k_pass] = codes
            plain_scales[k_pass] = scales

        v = const.tile([P, E * H1], F32)

        acc = {}
        mean_var = {}
        rstd = {}

        def norm_add(e):
            cols = slice(e * H1, (e + 1) * H1)
            nc.vector.tensor_tensor(out=v[:, cols], in0=acc[e][:], in1=bias_bc[:, cols], op=ALU.add)

        def norm_stats(e):
            stats = epi_pool.tile([P, 6], F32, name="stats")
            nc.vector.bn_stats(out=stats[:], in_=v[:, e * H1 : (e + 1) * H1])
            mean_var[e] = epi_pool.tile([P, 2], F32, name="mean_var")
            nc.vector.bn_aggr(out=mean_var[e][:], in_=stats[:])
            rstd[e] = epi_pool.tile([P, 1], F32, name="rstd")
            nc.gpsimd.tensor_scalar(
                out=rstd[e][:], in0=mean_var[e][:, 1:2], scalar1=EPS, scalar2=1.0, op0=ALU.add, op1=ALU.mult
            )
            nc.gpsimd.tensor_tensor(out=rstd[e][:], in0=rstd[e][:], in1=minus_half[:], op=ALU.pow)

        def norm_gain(e):
            cols = slice(e * H1, (e + 1) * H1)
            nc.vector.scalar_tensor_tensor(
                out=v[:, cols], in0=v[:, cols], scalar=mean_var[e][:, 0:1], in1=gain_bc[:, cols],
                op0=ALU.subtract, op1=ALU.mult,
            )

        def norm_shift(e):
            cols = slice(e * H1, (e + 1) * H1)
            nc.vector.scalar_tensor_tensor(
                out=v[:, cols], in0=v[:, cols], scalar=rstd[e][:], in1=shift_bc[:, cols],
                op0=ALU.mult, op1=ALU.add,
            )

        mish_scratch = {}

        def mish_begin():
            scratch = plain_keep.tile([P, 2, E * H1], F32, name="plain_grouped", align_bytes=64)
            mish_scratch["w"] = scratch[:, 0, :]
            mish_scratch["numer"] = scratch[:, 1, :]

        def mish_exp(cols):
            w_exp, numer = mish_scratch["w"], mish_scratch["numer"]
            nc.vector.tensor_scalar_min(out=w_exp[:, cols], in0=v[:, cols], scalar1=MISH_CLAMP)
            nc.scalar.activation(out=w_exp[:, cols], in_=w_exp[:, cols], func=ACT.Exp)

        def mish_numer(cols):
            w_exp, numer = mish_scratch["w"], mish_scratch["numer"]
            nc.vector.scalar_tensor_tensor(
                out=numer[:, cols], in0=w_exp[:, cols], scalar=2.0, in1=w_exp[:, cols], op0=ALU.add, op1=ALU.mult
            )

        def mish_denom(cols):
            w_exp, numer = mish_scratch["w"], mish_scratch["numer"]
            nc.vector.tensor_scalar_add(out=w_exp[:, cols], in0=numer[:, cols], scalar1=2.0)

        def mish_times_v(cols):
            w_exp, numer = mish_scratch["w"], mish_scratch["numer"]
            nc.vector.tensor_tensor(out=numer[:, cols], in0=numer[:, cols], in1=v[:, cols], op=ALU.mult)

        def mish_reciprocal(cols):
            w_exp, numer = mish_scratch["w"], mish_scratch["numer"]
            nc.vector.reciprocal(out=w_exp[:, cols], in_=w_exp[:, cols])

        def mish_store(first_e, last_e):
            w_exp, numer = mish_scratch["w"], mish_scratch["numer"]
            cols = slice(first_e * H1, last_e * H1)
            nc.vector.tensor_tensor(out=numer[:, cols], in0=numer[:, cols], in1=w_exp[:, cols], op=ALU.mult)
            nc.sync.dma_start(
                out=out[:, first_e:last_e, :].rearrange("b e h -> b (e h)"), in_=numer[:, cols]
            )

        turned = {}
        slot_grouped = {}
        slot_codes = {}
        slot_scales = {}

        def tokens_by_code(c, n):
            return tok[c][:, n, :].rearrange("p (w t) -> p t w", t=PACK)

        def new_term(c):
            term = term_pool.tile([P, PACK, CHUNK // PACK], F32, name="term")
            return term[:, :, : widths[c] // PACK]

        def vector_product(e, c, n):
            term = new_term(c)
            nc.vector.tensor_scalar_mul(out=term, in0=tokens_by_code(c, n), scalar1=disp[:, n, e : e + 1])
            return term

        def scalar_product(e, c, n):
            term = new_term(c)
            nc.scalar.activation(
                out=term.rearrange("p t (w i) -> p w t i", i=RUN),
                in_=tok[c][:, n, :].rearrange("p (w i t) -> p w t i", i=RUN, t=PACK),
                func=ACT.Copy, scale=disp[:, n, e : e + 1],
            )
            return term

        def vector_add(term, e, c, n):
            nc.vector.scalar_tensor_tensor(
                out=term, in0=tokens_by_code(c, n), scalar=disp[:, n, e : e + 1], in1=term,
                op0=ALU.mult, op1=ALU.add,
            )
            return term

        def transpose_term(term, e, c, opens, closes):
            for g in range(widths[c] // K_PASS):
                for t in range(PACK):
                    nc.tensor.matmul(
                        out=turned[e, c][g][:, t, :], lhsT=term[:, t, g * P : (g + 1) * P],
                        rhs=ident[:], is_transpose=True,
                        start=(opens and t == 0), stop=(closes and t == PACK - 1),
                    )

        def copy_slot(e, c, copies=(nc.scalar.copy, nc.scalar.copy)):
            grouped = slot_pool.tile([P, CHUNK_PASSES, B, PACK], BF16, name="grouped", align_bytes=64)
            for g in range(widths[c] // K_PASS):
                copies[g](out=grouped[:, g, :, :], in_=turned[e, c][g][:].rearrange("p t b -> p b t"))
            slot_grouped[e, c] = grouped

        def quantise_slot(e, c):
            passes = widths[c] // K_PASS
            codes = slot_pool.tile([P, CHUNK_PASSES * B], U32, name="s_codes", align_bytes=64, bufs=4)
            scales = slot_pool.tile([P, CHUNK_PASSES * B], U8, name="s_scales", align_bytes=64, bufs=4)
            nc.vector.quantize_mx(
                out=codes[:, : passes * B].bitcast(FP8X4),
                scales=scales[:, : passes * B],
                in_=slot_grouped[e, c][:, :passes, :, :].rearrange("p g b t -> p (g b t)"),
            )
            slot_codes[e, c] = codes
            slot_scales[e, c] = scales

        def multiply(e, k_pass, codes, scales, first_col, opens, closes):
            piece, w_pass = divmod(e * PASSES + k_pass, W_PASSES)
            cols = slice(first_col, first_col + B)
            w_cols = slice(w_pass * H1, (w_pass + 1) * H1)
            nc.tensor.matmul_mx(
                out=acc[e][:],
                lhsT=codes[:, cols].bitcast(FP8X4),
                lhsT_scale=scales[:, cols],
                rhs=w_codes[piece][:, w_cols].bitcast(FP8X4),
                rhs_scale=w_scales[piece][:, w_cols],
                start=opens,
                stop=closes,
            )

        def multiply_unit(e, c):
            last = c == last_chunk(e)
            if c == 0:
                acc[e] = acc_pool.tile([P, H1], F32, name="acc")
            if last:
                multiply(e, PASSES - 1, plain_codes[PASSES - 1], plain_scales[PASSES - 1], e * B, False, False)
                if e >= PLAIN_HALF_FROM:
                    multiply(
                        e, PASSES - 2, plain_codes[PASSES - 2], plain_scales[PASSES - 2],
                        (e - PLAIN_HALF_FROM) * B, False, False,
                    )
            passes = widths[c] // K_PASS
            for g in range(passes):
                multiply(
                    e, c * CHUNK_PASSES + g, slot_codes[e, c], slot_scales[e, c], g * B,
                    c == 0 and g == 0, last and g == passes - 1,
                )

        unread = unread_pool.tile([P, W_PASSES * H1], F32)

        def keep_warm(e, c):
            piece = (e * CHUNKS + c) // W_UNITS
            nc.tensor.matmul_mx(
                out=unread[:],
                lhsT=slot_codes[e, c][:, :B].bitcast(FP8X4),
                lhsT_scale=slot_scales[e, c][:, :B],
                rhs=w_codes[piece][:].bitcast(FP8X4),
                rhs_scale=w_scales[piece][:],
                start=True,
                stop=True,
            )

        def last_chunk(e):
            return CHUNKS - 1 if e < PLAIN_HALF_FROM else CHUNKS - 2

        units = [(e, c) for e in range(E) for c in range(last_chunk(e) + 1)]

        side = {}

        def put(i, q, func, *args):
            side.setdefault((i, q), []).append((func, args))

        for i, (e, c) in enumerate(units):
            if c % W_UNITS == 0:
                piece = (e * CHUNKS + c) // W_UNITS
                at = min(i + 2, len(units) - (1 if c == last_chunk(e) else 2))
                put(at, 0, regroup_w, piece)
                put(at, 2, quantise_w, piece)
                if 3 <= piece + 2 < W_PIECES:
                    put(at, 0, load_w, piece + 2)
            if c == last_chunk(e) and e < E - 1:
                put(i + 3, 1, norm_add, e)
                put(i + 3, 2, norm_stats, e)
                put(i + 4, 0, norm_gain, e)
                put(i + 4, 1, norm_shift, e)
            steps = []
            if e == 0 and c >= 4:
                steps = [2 * (c - 4), 2 * (c - 4) + 1]
            elif e == 1 and c >= 1:
                steps = [PLAIN_J, PLAIN_J + 1] if c == 1 else [PLAIN_J + c]
            for k, step in enumerate(steps):
                put(i, k, plain_cast, step)
                put(i, k + 1, plain_multiply, step)
                put(i + 1, k, plain_copy, step)
        first_of = {e: units.index((e, 0)) for e in range(E)}
        put(3, 0, make_diag)
        put(first_of[1] + 1, 0, plain_quantise, PASSES - 1, 0)
        put(first_of[2] + 1, 0, plain_quantise, PASSES - 2, PLAIN_HALF_FROM)
        tail = first_of[E - 1] + 4
        early = slice(0, (E - 1) * H1)
        put(tail, 0, mish_begin)
        put(tail, 0, mish_exp, early)
        put(tail + 1, 0, mish_numer, early)
        put(tail + 1, 1, mish_denom, early)
        put(tail + 1, 2, mish_times_v, early)
        put(tail + 2, 0, mish_reciprocal, slice(0, 4 * H1))
        put(tail + 2, 2, mish_store, 0, 4)

        for c in range(CHUNKS):
            for q in range(PAIRS):
                load_tokens(c, q)
            if c % W_UNITS == 1 and c // W_UNITS < 3:
                load_w(c // W_UNITS)
            if c in (4, 6):
                for step in range(4) if c == 4 else range(4, 6):
                    load_plain(step)
        with tc.manual_schedule():
            for i, (e, c) in enumerate(units):
                before = units[i - 2] if i >= 2 else None
                done = 0
                for q in range(PAIRS):
                    even, odd = 2 * q, 2 * q + 1
                    if before and q == 0:
                        copy_slot(*before)
                    if q == 2 or (q == 0 and c % 2 == 1):
                        terms = [scalar_product(e, c, even), vector_product(e, c, odd)]
                    elif q == 0:
                        terms = [vector_product(e, c, even), vector_product(e, c, odd)]
                    else:
                        terms = [vector_add(scalar_product(e, c, even), e, c, odd)]
                    if before and q == 1:
                        quantise_slot(*before)
                    if q == 0:
                        banks = [turned_pool.tile([P, PACK, B], F32, name="turned") for g in range(widths[c] // K_PASS)]
                        turned[e, c] = banks
                        if i >= 3:
                            multiply_unit(*units[i - 3])
                            keep_warm(*units[i - 3])
                            keep_warm(*units[i - 3])
                    for term in terms:
                        transpose_term(term, e, c, done == 0, q == PAIRS - 1)
                        done += 1
                    for func, args in side.get((i, q), []):
                        func(*args)
            multiply_unit(*units[-3])
            copy_slot(*units[-2])
            quantise_slot(*units[-2])
            multiply_unit(*units[-2])
            mish_reciprocal(slice(4 * H1, 6 * H1))
            copy_slot(*units[-1], copies=(nc.scalar.copy, nc.vector.tensor_copy))
            quantise_slot(*units[-1])
            multiply_unit(*units[-1])
            last = E - 1
            cols = slice(last * H1, E * H1)
            mish_reciprocal(slice(6 * H1, last * H1))
            norm_add(last)
            norm_stats(last)
            norm_gain(last)
            mish_store(4, last)
            norm_shift(last)
            mish_exp(cols)
            mish_numer(cols)
            mish_denom(cols)
            mish_times_v(cols)
            mish_reciprocal(cols)
            mish_store(last, E)
